import numpy as np
import ml_dtypes

BF16 = ml_dtypes.bfloat16


def bf(x):
    return np.asarray(x, np.float32).astype(BF16)


def f32(x):
    return np.asarray(x, np.float32)


def f64(x):
    return np.asarray(x).astype(np.float64)


def striped(idx):
    return np.tile(idx.reshape(-1, 16).T, (8, 1))


C, S, N, Q, M1, D = 256, 4096, 2048, 3, 256, 512
SCALE = np.sqrt(D)


def setup_inputs():
    pos = np.random.standard_normal((Q, N))
    pos[-1] = np.random.uniform(size=N)
    return {"x": f32(np.random.standard_normal((C, S))), "pos": f32(pos), "w_pos": f32(0.5 * np.random.standard_normal((C, Q))), "b0": f32(0.2 * np.random.standard_normal((C, 1))), "w1": bf(np.random.standard_normal((C, M1)) * np.sqrt(2.0 / C)), "b1": f32(0.2 * np.random.standard_normal((M1, 1))), "w2": bf(0.25 * np.random.standard_normal((M1, D)) / np.sqrt(M1)), "b2": f32(0.05 * np.random.standard_normal((D, 1))), "offs": striped(np.random.permutation(np.tile(np.arange(S), 2))[:N])}


def reference(x, pos, w_pos, b0, w1, b1, w2, b2, offs):
    idx = offs[:16].T.reshape(-1)
    wp, ps = f64(w_pos), f64(pos)
    other = f64(b0) + sum(wp[:, q:q + 1] * ps[q:q + 1] for q in range(Q))
    h0 = np.maximum(f64(x)[:, idx] + other, 0.0)
    h1 = np.maximum(f64(w1).T @ h0 + f64(b1), 0.0)
    return (f64(w2).T @ h1 + f64(b2)) * SCALE

@@ -1,0 +1,99 @@
+import math
+
+import concourse.mybir as mybir
+from concourse.masks import make_identity
+
+F32, BF16, U16 = mybir.dt.float32, mybir.dt.bfloat16, mybir.dt.uint16
+ADD, MULT = mybir.AluOpType.add, mybir.AluOpType.mult
+IDENTITY, RELU = mybir.ActivationFunctionType.Identity, mybir.ActivationFunctionType.Relu
+
+P = 128
+C, S, N, Q, M1, D = 256, 4096, 2048, 3, 256, 512
+SCALE = math.sqrt(D)
+CB, MB, DB = C // P, M1 // P, D // P
+PIECE = 512
+PIECES = N // PIECE
+FLOPS = 2 * N * (C * Q + C * M1 + M1 * D)
+
+
+def tile_baller2vec_kernel(tc, x, pos, w_pos, b0, w1, b1, w2, b2, offs, out):
+    nc = tc.nc
+    with (
+        tc.tile_pool(name="held", bufs=1) as held,
+        tc.tile_pool(name="work", bufs=3) as work,
+        tc.psum_pool(name="psum_other", bufs=2) as psum_other,
+        tc.psum_pool(name="psum_h1", bufs=2) as psum_h1,
+        tc.psum_pool(name="psum_out", bufs=4) as psum_out,
+    ):
+        offsets = held.tile([P, N // 16], U16, name="offsets")
+        nc.sync.dma_start(offsets[:], offs)
+        x_sb = [held.tile([P, S], F32, name=f"x_sb{b}") for b in range(CB)]
+        for b in range(CB):
+            nc.sync.dma_start(x_sb[b][:], x[b * P : (b + 1) * P, :])
+
+        pos_sb = held.tile([Q, N], F32, name="pos_sb")
+        nc.scalar.dma_start(pos_sb[:], pos)
+        wpos_sb = held.tile([P, CB, Q], F32, name="wpos_sb")
+        nc.scalar.dma_start(wpos_sb[:], w_pos.rearrange("(b p) q -> p b q", p=P))
+        b0_sb = held.tile([P, CB], F32, name="b0_sb")
+        b1_sb = held.tile([P, MB], F32, name="b1_sb")
+        b2_sb = held.tile([P, DB], F32, name="b2_sb")
+        with nc.allow_non_contiguous_dma(reason="a bias: one element to a partition"):
+            nc.scalar.dma_start(b0_sb[:], b0.rearrange("(b p) o -> p (b o)", p=P))
+            nc.scalar.dma_start(b1_sb[:], b1.rearrange("(b p) o -> p (b o)", p=P))
+            nc.scalar.dma_start(b2_sb[:], b2.rearrange("(b p) o -> p (b o)", p=P))
+        w1_sb = held.tile([P, CB, M1], BF16, name="w1_sb")
+        nc.scalar.dma_start(w1_sb[:], w1.rearrange("(b p) m -> p b m", p=P))
+        w2_sb = held.tile([P, MB, D], BF16, name="w2_sb")
+        nc.scalar.dma_start(w2_sb[:], w2.rearrange("(b p) d -> p b d", p=P))
+
+        b2_scaled = held.tile([P, DB], F32, name="b2_scaled")
+        nc.vector.tensor_scalar(b2_scaled[:], b2_sb[:], SCALE, None, MULT)
+
+        ident = held.tile([P, P], F32, name="ident")
+        make_identity(nc, ident[:])
+        wposT = held.tile([Q, C], F32, name="wposT")
+        for b in range(CB):
+            flipped = psum_other.tile([P, PIECE], F32, name="acc_other")
+            nc.tensor.transpose(flipped[:Q, :P], wpos_sb[:, b, :], ident[:])
+            nc.vector.tensor_copy(wposT[:, b * P : (b + 1) * P], flipped[:Q, :P])
+
+        other_sb = [held.tile([P, N], F32, name=f"other_sb{b}") for b in range(CB)]
+        for b in range(CB):
+            for p in range(PIECES):
+                cols = slice(p * PIECE, (p + 1) * PIECE)
+                acc_other = psum_other.tile([P, PIECE], F32, name="acc_other")
+                nc.tensor.matmul(acc_other[:], wposT[:, b * P : (b + 1) * P], pos_sb[:, cols], start=True, stop=True)
+                nc.scalar.activation(other_sb[b][:, cols], acc_other[:], IDENTITY, bias=b0_sb[:, b : b + 1])
+
+        for p in range(PIECES):
+            cols = slice(p * PIECE, (p + 1) * PIECE)
+            piece_offsets = offsets[:, p * (PIECE // 16) : (p + 1) * (PIECE // 16)]
+
+            h0 = work.tile([P, CB, PIECE], BF16, name="h0")
+            for b in range(CB):
+                summed = work.tile([P, PIECE], F32, name="summed")
+                nc.vector.tensor_tensor(summed[:], x_sb[b][:].indirect(piece_offsets), other_sb[b][:, cols], ADD)
+                nc.scalar.activation(h0[:, b, :], summed[:], RELU)
+
+            h1 = work.tile([P, MB, PIECE], BF16, name="h1")
+            for m in range(MB):
+                acc_h1 = psum_h1.tile([P, PIECE], F32, name="acc_h1")
+                for b in range(CB):
+                    nc.tensor.matmul(
+                        acc_h1[:], w1_sb[:, b, m * P : (m + 1) * P], h0[:, b, :], start=(b == 0), stop=(b == CB - 1)
+                    )
+                nc.scalar.activation(h1[:, m, :], acc_h1[:], RELU, bias=b1_sb[:, m : m + 1])
+
+            for d in range(DB):
+                acc_out = psum_out.tile([P, PIECE], F32, name="acc_out")
+                for m in range(MB):
+                    nc.tensor.matmul(
+                        acc_out[:], w2_sb[:, m, d * P : (d + 1) * P], h1[:, m, :], start=(m == 0), stop=(m == MB - 1)
+                    )
+                staged = work.tile([P, PIECE], F32, name="staged")
+                if d % 2 == 0:
+                    nc.scalar.activation(staged[:], acc_out[:], IDENTITY, bias=b2_scaled[:, d : d + 1], scale=SCALE)
+                else:
+                    nc.vector.tensor_scalar(staged[:], acc_out[:], SCALE, b2_scaled[:, d : d + 1], MULT, ADD)
+                nc.sync.dma_start(out[d * P : (d + 1) * P, cols], staged[:])

@@ -13,6 +13,7 @@ SCALE = math.sqrt(D)
 CB, MB, DB = C // P, M1 // P, D // P
 PIECE = 512
 PIECES = N // PIECE
+LEAD = 2
 FLOPS = 2 * N * (C * Q + C * M1 + M1 * D)
 
 
@@ -20,76 +21,80 @@ def tile_baller2vec_kernel(tc, x, pos, w_pos, b0, w1, b1, w2, b2, offs, out):
     nc = tc.nc
     with (
         tc.tile_pool(name="held", bufs=1) as held,
-        tc.tile_pool(name="work", bufs=3) as work,
+        tc.tile_pool(name="work", bufs=4) as work,
         tc.psum_pool(name="psum_other", bufs=2) as psum_other,
         tc.psum_pool(name="psum_h1", bufs=2) as psum_h1,
         tc.psum_pool(name="psum_out", bufs=4) as psum_out,
     ):
+        pos_pad = held.tile([P, N], F32, name="pos_pad")
+        nc.vector.memset(pos_pad[:], 0.0)
+        wposT_pad = held.tile([P, C], F32, name="wposT_pad")
+        nc.vector.memset(wposT_pad[:], 0.0)
+
         offsets = held.tile([P, N // 16], U16, name="offsets")
         nc.sync.dma_start(offsets[:], offs)
-        x_sb = [held.tile([P, S], F32, name=f"x_sb{b}") for b in range(CB)]
-        for b in range(CB):
-            nc.sync.dma_start(x_sb[b][:], x[b * P : (b + 1) * P, :])
-
-        pos_sb = held.tile([Q, N], F32, name="pos_sb")
-        nc.scalar.dma_start(pos_sb[:], pos)
         wpos_sb = held.tile([P, CB, Q], F32, name="wpos_sb")
-        nc.scalar.dma_start(wpos_sb[:], w_pos.rearrange("(b p) q -> p b q", p=P))
+        nc.sync.dma_start(wpos_sb[:], w_pos.rearrange("(b p) q -> p b q", p=P))
         b0_sb = held.tile([P, CB], F32, name="b0_sb")
         b1_sb = held.tile([P, MB], F32, name="b1_sb")
         b2_sb = held.tile([P, DB], F32, name="b2_sb")
         with nc.allow_non_contiguous_dma(reason="a bias: one element to a partition"):
-            nc.scalar.dma_start(b0_sb[:], b0.rearrange("(b p) o -> p (b o)", p=P))
-            nc.scalar.dma_start(b1_sb[:], b1.rearrange("(b p) o -> p (b o)", p=P))
-            nc.scalar.dma_start(b2_sb[:], b2.rearrange("(b p) o -> p (b o)", p=P))
+            nc.sync.dma_start(b0_sb[:], b0.rearrange("(b p) o -> p (b o)", p=P))
+        nc.sync.dma_start(pos_pad[:Q, :], pos)
+        x_sb = [held.tile([P, S], F32, name=f"x_sb{b}") for b in range(CB)]
+        for b in range(CB):
+            nc.sync.dma_start(x_sb[b][:], x[b * P : (b + 1) * P, :])
         w1_sb = held.tile([P, CB, M1], BF16, name="w1_sb")
-        nc.scalar.dma_start(w1_sb[:], w1.rearrange("(b p) m -> p b m", p=P))
+        nc.sync.dma_start(w1_sb[:], w1.rearrange("(b p) m -> p b m", p=P))
         w2_sb = held.tile([P, MB, D], BF16, name="w2_sb")
-        nc.scalar.dma_start(w2_sb[:], w2.rearrange("(b p) d -> p b d", p=P))
+        nc.sync.dma_start(w2_sb[:], w2.rearrange("(b p) d -> p b d", p=P))
+        with nc.allow_non_contiguous_dma(reason="a bias: one element to a partition"):
+            nc.sync.dma_start(b1_sb[:], b1.rearrange("(b p) o -> p (b o)", p=P))
+            nc.sync.dma_start(b2_sb[:], b2.rearrange("(b p) o -> p (b o)", p=P))
 
         b2_scaled = held.tile([P, DB], F32, name="b2_scaled")
-        nc.vector.tensor_scalar(b2_scaled[:], b2_sb[:], SCALE, None, MULT)
+        nc.gpsimd.tensor_scalar(b2_scaled[:], b2_sb[:], SCALE, None, MULT)
 
         ident = held.tile([P, P], F32, name="ident")
         make_identity(nc, ident[:])
-        wposT = held.tile([Q, C], F32, name="wposT")
         for b in range(CB):
             flipped = psum_other.tile([P, PIECE], F32, name="acc_other")
             nc.tensor.transpose(flipped[:Q, :P], wpos_sb[:, b, :], ident[:])
-            nc.vector.tensor_copy(wposT[:, b * P : (b + 1) * P], flipped[:Q, :P])
+            nc.vector.tensor_copy(wposT_pad[:Q, b * P : (b + 1) * P], flipped[:Q, :P])
 
         other_sb = [held.tile([P, N], F32, name=f"other_sb{b}") for b in range(CB)]
-        for b in range(CB):
-            for p in range(PIECES):
-                cols = slice(p * PIECE, (p + 1) * PIECE)
-                acc_other = psum_other.tile([P, PIECE], F32, name="acc_other")
-                nc.tensor.matmul(acc_other[:], wposT[:, b * P : (b + 1) * P], pos_sb[:, cols], start=True, stop=True)
-                nc.scalar.activation(other_sb[b][:, cols], acc_other[:], IDENTITY, bias=b0_sb[:, b : b + 1])
+        h0 = [held.tile([P, CB, PIECE], BF16, name=f"h0_{p}") for p in range(PIECES)]
+        h1 = [held.tile([P, MB, PIECE], BF16, name=f"h1_{p}") for p in range(PIECES)]
 
-        for p in range(PIECES):
+        def make_other(b, p):
+            cols = slice(p * PIECE, (p + 1) * PIECE)
+            acc_other = psum_other.tile([P, PIECE], F32, name="acc_other")
+            nc.tensor.matmul(acc_other[:], wposT_pad[:, b * P : (b + 1) * P], pos_pad[:, cols], start=True, stop=True)
+            nc.scalar.activation(other_sb[b][:, cols], acc_other[:], IDENTITY, bias=b0_sb[:, b : b + 1])
+
+        def look_up(b, p):
             cols = slice(p * PIECE, (p + 1) * PIECE)
             piece_offsets = offsets[:, p * (PIECE // 16) : (p + 1) * (PIECE // 16)]
+            summed = work.tile([P, PIECE], F32, name="summed")
+            nc.vector.tensor_tensor(summed[:], x_sb[b][:].indirect(piece_offsets), other_sb[b][:, cols], ADD)
+            nc.scalar.activation(h0[p][:, b, :], summed[:], RELU)
 
-            h0 = work.tile([P, CB, PIECE], BF16, name="h0")
-            for b in range(CB):
-                summed = work.tile([P, PIECE], F32, name="summed")
-                nc.vector.tensor_tensor(summed[:], x_sb[b][:].indirect(piece_offsets), other_sb[b][:, cols], ADD)
-                nc.scalar.activation(h0[:, b, :], summed[:], RELU)
-
-            h1 = work.tile([P, MB, PIECE], BF16, name="h1")
+        def layer1(p):
             for m in range(MB):
                 acc_h1 = psum_h1.tile([P, PIECE], F32, name="acc_h1")
                 for b in range(CB):
                     nc.tensor.matmul(
-                        acc_h1[:], w1_sb[:, b, m * P : (m + 1) * P], h0[:, b, :], start=(b == 0), stop=(b == CB - 1)
+                        acc_h1[:], w1_sb[:, b, m * P : (m + 1) * P], h0[p][:, b, :], start=(b == 0), stop=(b == CB - 1)
                     )
-                nc.scalar.activation(h1[:, m, :], acc_h1[:], RELU, bias=b1_sb[:, m : m + 1])
+                nc.scalar.activation(h1[p][:, m, :], acc_h1[:], RELU, bias=b1_sb[:, m : m + 1])
 
+        def layer2(p):
+            cols = slice(p * PIECE, (p + 1) * PIECE)
             for d in range(DB):
                 acc_out = psum_out.tile([P, PIECE], F32, name="acc_out")
                 for m in range(MB):
                     nc.tensor.matmul(
-                        acc_out[:], w2_sb[:, m, d * P : (d + 1) * P], h1[:, m, :], start=(m == 0), stop=(m == MB - 1)
+                        acc_out[:], w2_sb[:, m, d * P : (d + 1) * P], h1[p][:, m, :], start=(m == 0), stop=(m == MB - 1)
                     )
                 staged = work.tile([P, PIECE], F32, name="staged")
                 if d % 2 == 0:
@@ -97,3 +102,16 @@ def tile_baller2vec_kernel(tc, x, pos, w_pos, b0, w1, b1, w2, b2, offs, out):
                 else:
                     nc.vector.tensor_scalar(staged[:], acc_out[:], SCALE, b2_scaled[:, d : d + 1], MULT, ADD)
                 nc.sync.dma_start(out[d * P : (d + 1) * P, cols], staged[:])
+
+        units = [(b, p) for b in range(CB) for p in range(PIECES)]
+        for u in range(LEAD):
+            make_other(*units[u])
+        for u, (b, p) in enumerate(units):
+            if u + LEAD < len(units):
+                make_other(*units[u + LEAD])
+            look_up(b, p)
+            if b == CB - 1:
+                layer1(p)
+                if p > 0:
+                    layer2(p - 1)
+        layer2(PIECES - 1)

@@ -4,7 +4,7 @@ import concourse.mybir as mybir
 from concourse.masks import make_identity
 
 F32, BF16, U16 = mybir.dt.float32, mybir.dt.bfloat16, mybir.dt.uint16
-ADD, MULT = mybir.AluOpType.add, mybir.AluOpType.mult
+ADD, MULT, MAX = mybir.AluOpType.add, mybir.AluOpType.mult, mybir.AluOpType.max
 IDENTITY, RELU = mybir.ActivationFunctionType.Identity, mybir.ActivationFunctionType.Relu
 
 P = 128
@@ -13,7 +13,6 @@ SCALE = math.sqrt(D)
 CB, MB, DB = C // P, M1 // P, D // P
 PIECE = 512
 PIECES = N // PIECE
-LEAD = 2
 FLOPS = 2 * N * (C * Q + C * M1 + M1 * D)
 
 
@@ -22,6 +21,7 @@ def tile_baller2vec_kernel(tc, x, pos, w_pos, b0, w1, b1, w2, b2, offs, out):
     with (
         tc.tile_pool(name="held", bufs=1) as held,
         tc.tile_pool(name="work", bufs=4) as work,
+        tc.tile_pool(name="stage", bufs=8) as stage,
         tc.psum_pool(name="psum_other", bufs=2) as psum_other,
         tc.psum_pool(name="psum_h1", bufs=2) as psum_h1,
         tc.psum_pool(name="psum_out", bufs=4) as psum_out,
@@ -35,12 +35,13 @@ def tile_baller2vec_kernel(tc, x, pos, w_pos, b0, w1, b1, w2, b2, offs, out):
         nc.sync.dma_start(offsets[:], offs)
         wpos_sb = held.tile([P, CB, Q], F32, name="wpos_sb")
         nc.sync.dma_start(wpos_sb[:], w_pos.rearrange("(b p) q -> p b q", p=P))
+        pos_sb = held.tile([Q, N], F32, name="pos_sb")
+        nc.sync.dma_start(pos_sb[:], pos)
         b0_sb = held.tile([P, CB], F32, name="b0_sb")
         b1_sb = held.tile([P, MB], F32, name="b1_sb")
         b2_sb = held.tile([P, DB], F32, name="b2_sb")
         with nc.allow_non_contiguous_dma(reason="a bias: one element to a partition"):
             nc.sync.dma_start(b0_sb[:], b0.rearrange("(b p) o -> p (b o)", p=P))
-        nc.sync.dma_start(pos_pad[:Q, :], pos)
         x_sb = [held.tile([P, S], F32, name=f"x_sb{b}") for b in range(CB)]
         for b in range(CB):
             nc.sync.dma_start(x_sb[b][:], x[b * P : (b + 1) * P, :])
@@ -62,6 +63,10 @@ def tile_baller2vec_kernel(tc, x, pos, w_pos, b0, w1, b1, w2, b2, offs, out):
             nc.tensor.transpose(flipped[:Q, :P], wpos_sb[:, b, :], ident[:])
             nc.vector.tensor_copy(wposT_pad[:Q, b * P : (b + 1) * P], flipped[:Q, :P])
 
+        for p in range(PIECES):
+            cols = slice(p * PIECE, (p + 1) * PIECE)
+            nc.vector.tensor_copy(pos_pad[:Q, cols], pos_sb[:, cols])
+
         other_sb = [held.tile([P, N], F32, name=f"other_sb{b}") for b in range(CB)]
         h0 = [held.tile([P, CB, PIECE], BF16, name=f"h0_{p}") for p in range(PIECES)]
         h1 = [held.tile([P, MB, PIECE], BF16, name=f"h1_{p}") for p in range(PIECES)]
@@ -77,7 +82,10 @@ def tile_baller2vec_kernel(tc, x, pos, w_pos, b0, w1, b1, w2, b2, offs, out):
             piece_offsets = offsets[:, p * (PIECE // 16) : (p + 1) * (PIECE // 16)]
             summed = work.tile([P, PIECE], F32, name="summed")
             nc.vector.tensor_tensor(summed[:], x_sb[b][:].indirect(piece_offsets), other_sb[b][:, cols], ADD)
-            nc.scalar.activation(h0[p][:, b, :], summed[:], RELU)
+            if b == 0:
+                nc.scalar.activation(h0[p][:, b, :], summed[:], RELU)
+            else:
+                nc.vector.tensor_scalar(h0[p][:, b, :], summed[:], 0.0, None, MAX)
 
         def layer1(p):
             for m in range(MB):
@@ -96,22 +104,22 @@ def tile_baller2vec_kernel(tc, x, pos, w_pos, b0, w1, b1, w2, b2, offs, out):
                     nc.tensor.matmul(
                         acc_out[:], w2_sb[:, m, d * P : (d + 1) * P], h1[p][:, m, :], start=(m == 0), stop=(m == MB - 1)
                     )
-                staged = work.tile([P, PIECE], F32, name="staged")
+                staged = stage.tile([P, PIECE], F32, name="staged")
                 if d % 2 == 0:
                     nc.scalar.activation(staged[:], acc_out[:], IDENTITY, bias=b2_scaled[:, d : d + 1], scale=SCALE)
                 else:
                     nc.vector.tensor_scalar(staged[:], acc_out[:], SCALE, b2_scaled[:, d : d + 1], MULT, ADD)
                 nc.sync.dma_start(out[d * P : (d + 1) * P, cols], staged[:])
 
-        units = [(b, p) for b in range(CB) for p in range(PIECES)]
-        for u in range(LEAD):
-            make_other(*units[u])
-        for u, (b, p) in enumerate(units):
-            if u + LEAD < len(units):
-                make_other(*units[u + LEAD])
-            look_up(b, p)
-            if b == CB - 1:
-                layer1(p)
-                if p > 0:
-                    layer2(p - 1)
-        layer2(PIECES - 1)
+        for p in range(PIECES):
+            make_other(0, p)
+        for p in range(PIECES):
+            look_up(0, p)
+            make_other(1, p)
+        for step in range(PIECES + 2):
+            if step < PIECES:
+                look_up(1, step)
+            if 1 <= step <= PIECES:
+                layer1(step - 1)
+            if step >= 2:
+                layer2(step - 2)

@@ -22,9 +22,7 @@ def tile_baller2vec_kernel(tc, x, pos, w_pos, b0, w1, b1, w2, b2, offs, out):
         tc.tile_pool(name="held", bufs=1) as held,
         tc.tile_pool(name="work", bufs=4) as work,
         tc.tile_pool(name="stage", bufs=8) as stage,
-        tc.psum_pool(name="psum_other", bufs=2) as psum_other,
-        tc.psum_pool(name="psum_h1", bufs=2) as psum_h1,
-        tc.psum_pool(name="psum_out", bufs=4) as psum_out,
+        tc.psum_pool(name="psum", bufs=8) as psum,
     ):
         pos_pad = held.tile([P, N], F32, name="pos_pad")
         nc.vector.memset(pos_pad[:], 0.0)
@@ -43,10 +41,10 @@ def tile_baller2vec_kernel(tc, x, pos, w_pos, b0, w1, b1, w2, b2, offs, out):
         with nc.allow_non_contiguous_dma(reason="a bias: one element to a partition"):
             nc.sync.dma_start(b0_sb[:], b0.rearrange("(b p) o -> p (b o)", p=P))
         x_sb = [held.tile([P, S], F32, name=f"x_sb{b}") for b in range(CB)]
-        for b in range(CB):
-            nc.sync.dma_start(x_sb[b][:], x[b * P : (b + 1) * P, :])
+        nc.sync.dma_start(x_sb[0][:], x[0:P, :])
         w1_sb = held.tile([P, CB, M1], BF16, name="w1_sb")
         nc.sync.dma_start(w1_sb[:], w1.rearrange("(b p) m -> p b m", p=P))
+        nc.sync.dma_start(x_sb[1][:], x[P : 2 * P, :])
         w2_sb = held.tile([P, MB, D], BF16, name="w2_sb")
         nc.sync.dma_start(w2_sb[:], w2.rearrange("(b p) d -> p b d", p=P))
         with nc.allow_non_contiguous_dma(reason="a bias: one element to a partition"):
@@ -59,7 +57,7 @@ def tile_baller2vec_kernel(tc, x, pos, w_pos, b0, w1, b1, w2, b2, offs, out):
         ident = held.tile([P, P], F32, name="ident")
         make_identity(nc, ident[:])
         for b in range(CB):
-            flipped = psum_other.tile([P, PIECE], F32, name="acc_other")
+            flipped = psum.tile([P, PIECE], F32, name="bank")
             nc.tensor.transpose(flipped[:Q, :P], wpos_sb[:, b, :], ident[:])
             nc.vector.tensor_copy(wposT_pad[:Q, b * P : (b + 1) * P], flipped[:Q, :P])
 
@@ -73,7 +71,7 @@ def tile_baller2vec_kernel(tc, x, pos, w_pos, b0, w1, b1, w2, b2, offs, out):
 
         def make_other(b, p):
             cols = slice(p * PIECE, (p + 1) * PIECE)
-            acc_other = psum_other.tile([P, PIECE], F32, name="acc_other")
+            acc_other = psum.tile([P, PIECE], F32, name="bank")
             nc.tensor.matmul(acc_other[:], wposT_pad[:, b * P : (b + 1) * P], pos_pad[:, cols], start=True, stop=True)
             nc.scalar.activation(other_sb[b][:, cols], acc_other[:], IDENTITY, bias=b0_sb[:, b : b + 1])
 
@@ -87,19 +85,22 @@ def tile_baller2vec_kernel(tc, x, pos, w_pos, b0, w1, b1, w2, b2, offs, out):
             else:
                 nc.vector.tensor_scalar(h0[p][:, b, :], summed[:], 0.0, None, MAX)
 
-        def layer1(p):
+        acc_h1 = {}
+
+        def layer1_begin(p):
             for m in range(MB):
-                acc_h1 = psum_h1.tile([P, PIECE], F32, name="acc_h1")
-                for b in range(CB):
-                    nc.tensor.matmul(
-                        acc_h1[:], w1_sb[:, b, m * P : (m + 1) * P], h0[p][:, b, :], start=(b == 0), stop=(b == CB - 1)
-                    )
-                nc.scalar.activation(h1[p][:, m, :], acc_h1[:], RELU, bias=b1_sb[:, m : m + 1])
+                acc_h1[p, m] = psum.tile([P, PIECE], F32, name="bank")
+                nc.tensor.matmul(acc_h1[p, m][:], w1_sb[:, 0, m * P : (m + 1) * P], h0[p][:, 0, :], start=True, stop=False)
+
+        def layer1_end(p):
+            for m in range(MB):
+                nc.tensor.matmul(acc_h1[p, m][:], w1_sb[:, 1, m * P : (m + 1) * P], h0[p][:, 1, :], start=False, stop=True)
+                nc.scalar.activation(h1[p][:, m, :], acc_h1[p, m][:], RELU, bias=b1_sb[:, m : m + 1])
 
         def layer2(p):
             cols = slice(p * PIECE, (p + 1) * PIECE)
             for d in range(DB):
-                acc_out = psum_out.tile([P, PIECE], F32, name="acc_out")
+                acc_out = psum.tile([P, PIECE], F32, name="bank")
                 for m in range(MB):
                     nc.tensor.matmul(
                         acc_out[:], w2_sb[:, m, d * P : (d + 1) * P], h1[p][:, m, :], start=(m == 0), stop=(m == MB - 1)
@@ -116,10 +117,12 @@ def tile_baller2vec_kernel(tc, x, pos, w_pos, b0, w1, b1, w2, b2, offs, out):
         for p in range(PIECES):
             look_up(0, p)
             make_other(1, p)
+        for p in range(PIECES):
+            layer1_begin(p)
         for step in range(PIECES + 2):
             if step < PIECES:
                 look_up(1, step)
             if 1 <= step <= PIECES:
-                layer1(step - 1)
+                layer1_end(step - 1)
             if step >= 2:
                 layer2(step - 2)

@@ -13,6 +13,7 @@ SCALE = math.sqrt(D)
 CB, MB, DB = C // P, M1 // P, D // P
 PIECE = 512
 PIECES = N // PIECE
+WARM_UP = 8
 FLOPS = 2 * N * (C * Q + C * M1 + M1 * D)
 
 
@@ -29,12 +30,18 @@ def tile_baller2vec_kernel(tc, x, pos, w_pos, b0, w1, b1, w2, b2, offs, out):
         wposT_pad = held.tile([P, C], F32, name="wposT_pad")
         nc.vector.memset(wposT_pad[:], 0.0)
 
+        zeros = held.tile([P, PIECE], BF16, name="zeros")
+        nc.gpsimd.memset(zeros[:], 0.0)
+        for i in range(WARM_UP):
+            unused = psum.tile([P, PIECE], F32, name="bank")
+            nc.tensor.matmul(unused[:], zeros[:, :P], zeros[:], start=True, stop=True)
+
         offsets = held.tile([P, N // 16], U16, name="offsets")
         nc.sync.dma_start(offsets[:], offs)
-        wpos_sb = held.tile([P, CB, Q], F32, name="wpos_sb")
-        nc.sync.dma_start(wpos_sb[:], w_pos.rearrange("(b p) q -> p b q", p=P))
         pos_sb = held.tile([Q, N], F32, name="pos_sb")
         nc.sync.dma_start(pos_sb[:], pos)
+        wpos_sb = held.tile([P, CB, Q], F32, name="wpos_sb")
+        nc.sync.dma_start(wpos_sb[:], w_pos.rearrange("(b p) q -> p b q", p=P))
         b0_sb = held.tile([P, CB], F32, name="b0_sb")
         b1_sb = held.tile([P, MB], F32, name="b1_sb")
         b2_sb = held.tile([P, DB], F32, name="b2_sb")
@@ -66,7 +73,7 @@ def tile_baller2vec_kernel(tc, x, pos, w_pos, b0, w1, b1, w2, b2, offs, out):
             nc.vector.tensor_copy(pos_pad[:Q, cols], pos_sb[:, cols])
 
         other_sb = [held.tile([P, N], F32, name=f"other_sb{b}") for b in range(CB)]
-        h0 = [held.tile([P, CB, PIECE], BF16, name=f"h0_{p}") for p in range(PIECES)]
+        h0 = [[held.tile([P, PIECE], BF16, name=f"h0_{b}_{p}") for p in range(PIECES)] for b in range(CB)]
         h1 = [held.tile([P, MB, PIECE], BF16, name=f"h1_{p}") for p in range(PIECES)]
 
         def make_other(b, p):
@@ -81,20 +88,20 @@ def tile_baller2vec_kernel(tc, x, pos, w_pos, b0, w1, b1, w2, b2, offs, out):
             summed = work.tile([P, PIECE], F32, name="summed")
             nc.vector.tensor_tensor(summed[:], x_sb[b][:].indirect(piece_offsets), other_sb[b][:, cols], ADD)
             if b == 0:
-                nc.scalar.activation(h0[p][:, b, :], summed[:], RELU)
+                nc.scalar.activation(h0[b][p][:], summed[:], RELU)
             else:
-                nc.vector.tensor_scalar(h0[p][:, b, :], summed[:], 0.0, None, MAX)
+                nc.vector.tensor_scalar(h0[b][p][:], summed[:], 0.0, None, MAX)
 
         acc_h1 = {}
 
         def layer1_begin(p):
             for m in range(MB):
                 acc_h1[p, m] = psum.tile([P, PIECE], F32, name="bank")
-                nc.tensor.matmul(acc_h1[p, m][:], w1_sb[:, 0, m * P : (m + 1) * P], h0[p][:, 0, :], start=True, stop=False)
+                nc.tensor.matmul(acc_h1[p, m][:], w1_sb[:, 0, m * P : (m + 1) * P], h0[0][p][:], start=True, stop=False)
 
         def layer1_end(p):
             for m in range(MB):
-                nc.tensor.matmul(acc_h1[p, m][:], w1_sb[:, 1, m * P : (m + 1) * P], h0[p][:, 1, :], start=False, stop=True)
+                nc.tensor.matmul(acc_h1[p, m][:], w1_sb[:, 1, m * P : (m + 1) * P], h0[1][p][:], start=False, stop=True)
                 nc.scalar.activation(h1[p][:, m, :], acc_h1[p, m][:], RELU, bias=b1_sb[:, m : m + 1])
 
         def layer2(p):

@@ -13,7 +13,8 @@ SCALE = math.sqrt(D)
 CB, MB, DB = C // P, M1 // P, D // P
 PIECE = 512
 PIECES = N // PIECE
-WARM_UP = 8
+WARM_UP_LOADS = 3
+WARM_UP_COPIES = 2
 FLOPS = 2 * N * (C * Q + C * M1 + M1 * D)
 
 
@@ -32,16 +33,20 @@ def tile_baller2vec_kernel(tc, x, pos, w_pos, b0, w1, b1, w2, b2, offs, out):
 
         zeros = held.tile([P, PIECE], BF16, name="zeros")
         nc.gpsimd.memset(zeros[:], 0.0)
-        for i in range(WARM_UP):
-            unused = psum.tile([P, PIECE], F32, name="bank")
-            nc.tensor.matmul(unused[:], zeros[:, :P], zeros[:], start=True, stop=True)
+
+        def multiply_zeros(times):
+            for i in range(times):
+                unused = psum.tile([P, PIECE], F32, name="bank")
+                nc.tensor.matmul(unused[:], zeros[:, :P], zeros[:], start=True, stop=True)
+
+        multiply_zeros(WARM_UP_LOADS)
 
         offsets = held.tile([P, N // 16], U16, name="offsets")
         nc.sync.dma_start(offsets[:], offs)
-        pos_sb = held.tile([Q, N], F32, name="pos_sb")
-        nc.sync.dma_start(pos_sb[:], pos)
         wpos_sb = held.tile([P, CB, Q], F32, name="wpos_sb")
         nc.sync.dma_start(wpos_sb[:], w_pos.rearrange("(b p) q -> p b q", p=P))
+        pos_sb = held.tile([Q, N], F32, name="pos_sb")
+        nc.sync.dma_start(pos_sb[:], pos)
         b0_sb = held.tile([P, CB], F32, name="b0_sb")
         b1_sb = held.tile([P, MB], F32, name="b1_sb")
         b2_sb = held.tile([P, DB], F32, name="b2_sb")
@@ -58,19 +63,20 @@ def tile_baller2vec_kernel(tc, x, pos, w_pos, b0, w1, b1, w2, b2, offs, out):
             nc.sync.dma_start(b1_sb[:], b1.rearrange("(b p) o -> p (b o)", p=P))
             nc.sync.dma_start(b2_sb[:], b2.rearrange("(b p) o -> p (b o)", p=P))
 
-        b2_scaled = held.tile([P, DB], F32, name="b2_scaled")
-        nc.gpsimd.tensor_scalar(b2_scaled[:], b2_sb[:], SCALE, None, MULT)
-
         ident = held.tile([P, P], F32, name="ident")
         make_identity(nc, ident[:])
         for b in range(CB):
             flipped = psum.tile([P, PIECE], F32, name="bank")
             nc.tensor.transpose(flipped[:Q, :P], wpos_sb[:, b, :], ident[:])
             nc.vector.tensor_copy(wposT_pad[:Q, b * P : (b + 1) * P], flipped[:Q, :P])
+        multiply_zeros(WARM_UP_COPIES)
 
         for p in range(PIECES):
             cols = slice(p * PIECE, (p + 1) * PIECE)
             nc.vector.tensor_copy(pos_pad[:Q, cols], pos_sb[:, cols])
+
+        b2_scaled = held.tile([P, DB], F32, name="b2_scaled")
+        nc.gpsimd.tensor_scalar(b2_scaled[:], b2_sb[:], SCALE, None, MULT)
 
         other_sb = [held.tile([P, N], F32, name=f"other_sb{b}") for b in range(CB)]
         h0 = [[held.tile([P, PIECE], BF16, name=f"h0_{b}_{p}") for p in range(PIECES)] for b in range(CB)]

@@ -13,8 +13,7 @@ SCALE = math.sqrt(D)
 CB, MB, DB = C // P, M1 // P, D // P
 PIECE = 512
 PIECES = N // PIECE
-WARM_UP_LOADS = 3
-WARM_UP_COPIES = 2
+WARM_UP = 8
 FLOPS = 2 * N * (C * Q + C * M1 + M1 * D)
 
 
@@ -33,20 +32,16 @@ def tile_baller2vec_kernel(tc, x, pos, w_pos, b0, w1, b1, w2, b2, offs, out):
 
         zeros = held.tile([P, PIECE], BF16, name="zeros")
         nc.gpsimd.memset(zeros[:], 0.0)
-
-        def multiply_zeros(times):
-            for i in range(times):
-                unused = psum.tile([P, PIECE], F32, name="bank")
-                nc.tensor.matmul(unused[:], zeros[:, :P], zeros[:], start=True, stop=True)
-
-        multiply_zeros(WARM_UP_LOADS)
+        for i in range(WARM_UP):
+            unused = psum.tile([P, PIECE], F32, name="bank")
+            nc.tensor.matmul(unused[:], zeros[:, :P], zeros[:], start=True, stop=True)
 
         offsets = held.tile([P, N // 16], U16, name="offsets")
         nc.sync.dma_start(offsets[:], offs)
-        wpos_sb = held.tile([P, CB, Q], F32, name="wpos_sb")
-        nc.sync.dma_start(wpos_sb[:], w_pos.rearrange("(b p) q -> p b q", p=P))
         pos_sb = held.tile([Q, N], F32, name="pos_sb")
         nc.sync.dma_start(pos_sb[:], pos)
+        wpos_sb = held.tile([P, CB, Q], F32, name="wpos_sb")
+        nc.sync.dma_start(wpos_sb[:], w_pos.rearrange("(b p) q -> p b q", p=P))
         b0_sb = held.tile([P, CB], F32, name="b0_sb")
         b1_sb = held.tile([P, MB], F32, name="b1_sb")
         b2_sb = held.tile([P, DB], F32, name="b2_sb")
@@ -63,20 +58,19 @@ def tile_baller2vec_kernel(tc, x, pos, w_pos, b0, w1, b1, w2, b2, offs, out):
             nc.sync.dma_start(b1_sb[:], b1.rearrange("(b p) o -> p (b o)", p=P))
             nc.sync.dma_start(b2_sb[:], b2.rearrange("(b p) o -> p (b o)", p=P))
 
+        b2_scaled = held.tile([P, DB], F32, name="b2_scaled")
+        nc.gpsimd.tensor_scalar(b2_scaled[:], b2_sb[:], SCALE, None, MULT)
+
         ident = held.tile([P, P], F32, name="ident")
         make_identity(nc, ident[:])
         for b in range(CB):
             flipped = psum.tile([P, PIECE], F32, name="bank")
             nc.tensor.transpose(flipped[:Q, :P], wpos_sb[:, b, :], ident[:])
             nc.vector.tensor_copy(wposT_pad[:Q, b * P : (b + 1) * P], flipped[:Q, :P])
-        multiply_zeros(WARM_UP_COPIES)
 
         for p in range(PIECES):
             cols = slice(p * PIECE, (p + 1) * PIECE)
             nc.vector.tensor_copy(pos_pad[:Q, cols], pos_sb[:, cols])
-
-        b2_scaled = held.tile([P, DB], F32, name="b2_scaled")
-        nc.gpsimd.tensor_scalar(b2_scaled[:], b2_sb[:], SCALE, None, MULT)
 
         other_sb = [held.tile([P, N], F32, name=f"other_sb{b}") for b in range(CB)]
         h0 = [[held.tile([P, PIECE], BF16, name=f"h0_{b}_{p}") for p in range(PIECES)] for b in range(CB)]
@@ -98,17 +92,14 @@ def tile_baller2vec_kernel(tc, x, pos, w_pos, b0, w1, b1, w2, b2, offs, out):
             else:
                 nc.vector.tensor_scalar(h0[b][p][:], summed[:], 0.0, None, MAX)
 
-        acc_h1 = {}
-
-        def layer1_begin(p):
+        def layer1(p):
             for m in range(MB):
-                acc_h1[p, m] = psum.tile([P, PIECE], F32, name="bank")
-                nc.tensor.matmul(acc_h1[p, m][:], w1_sb[:, 0, m * P : (m + 1) * P], h0[0][p][:], start=True, stop=False)
-
-        def layer1_end(p):
-            for m in range(MB):
-                nc.tensor.matmul(acc_h1[p, m][:], w1_sb[:, 1, m * P : (m + 1) * P], h0[1][p][:], start=False, stop=True)
-                nc.scalar.activation(h1[p][:, m, :], acc_h1[p, m][:], RELU, bias=b1_sb[:, m : m + 1])
+                acc_h1 = psum.tile([P, PIECE], F32, name="bank")
+                for b in range(CB):
+                    nc.tensor.matmul(
+                        acc_h1[:], w1_sb[:, b, m * P : (m + 1) * P], h0[b][p][:], start=(b == 0), stop=(b == CB - 1)
+                    )
+                nc.scalar.activation(h1[p][:, m, :], acc_h1[:], RELU, bias=b1_sb[:, m : m + 1])
 
         def layer2(p):
             cols = slice(p * PIECE, (p + 1) * PIECE)
@@ -130,12 +121,10 @@ def tile_baller2vec_kernel(tc, x, pos, w_pos, b0, w1, b1, w2, b2, offs, out):
         for p in range(PIECES):
             look_up(0, p)
             make_other(1, p)
-        for p in range(PIECES):
-            layer1_begin(p)
         for step in range(PIECES + 2):
             if step < PIECES:
                 look_up(1, step)
             if 1 <= step <= PIECES:
-                layer1_end(step - 1)
+                layer1(step - 1)
             if step >= 2:
                 layer2(step - 2)

@@ -92,14 +92,17 @@ def tile_baller2vec_kernel(tc, x, pos, w_pos, b0, w1, b1, w2, b2, offs, out):
             else:
                 nc.vector.tensor_scalar(h0[b][p][:], summed[:], 0.0, None, MAX)
 
-        def layer1(p):
+        acc_h1 = {}
+
+        def layer1_block0(p):
+            acc_h1[p] = [psum.tile([P, PIECE], F32, name="bank") for m in range(MB)]
             for m in range(MB):
-                acc_h1 = psum.tile([P, PIECE], F32, name="bank")
-                for b in range(CB):
-                    nc.tensor.matmul(
-                        acc_h1[:], w1_sb[:, b, m * P : (m + 1) * P], h0[b][p][:], start=(b == 0), stop=(b == CB - 1)
-                    )
-                nc.scalar.activation(h1[p][:, m, :], acc_h1[:], RELU, bias=b1_sb[:, m : m + 1])
+                nc.tensor.matmul(acc_h1[p][m][:], w1_sb[:, 0, m * P : (m + 1) * P], h0[0][p][:], start=True, stop=False)
+
+        def layer1_block1(p):
+            for m in range(MB):
+                nc.tensor.matmul(acc_h1[p][m][:], w1_sb[:, 1, m * P : (m + 1) * P], h0[1][p][:], start=False, stop=True)
+                nc.scalar.activation(h1[p][:, m, :], acc_h1[p][m][:], RELU, bias=b1_sb[:, m : m + 1])
 
         def layer2(p):
             cols = slice(p * PIECE, (p + 1) * PIECE)
@@ -121,10 +124,13 @@ def tile_baller2vec_kernel(tc, x, pos, w_pos, b0, w1, b1, w2, b2, offs, out):
         for p in range(PIECES):
             look_up(0, p)
             make_other(1, p)
-        for step in range(PIECES + 2):
+        layer1_block0(0)
+        layer1_block0(1)
+        for step in range(PIECES + 1):
             if step < PIECES:
                 look_up(1, step)
-            if 1 <= step <= PIECES:
-                layer1(step - 1)
-            if step >= 2:
-                layer2(step - 2)
+                layer1_block1(step)
+            if step + 2 < PIECES:
+                layer1_block0(step + 2)
+            if step >= 1:
+                layer2(step - 1)

@@ -13,7 +13,7 @@ SCALE = math.sqrt(D)
 CB, MB, DB = C // P, M1 // P, D // P
 PIECE = 512
 PIECES = N // PIECE
-WARM_UP = 8
+WARM_UP = 4
 FLOPS = 2 * N * (C * Q + C * M1 + M1 * D)
 
 
@@ -61,16 +61,16 @@ def tile_baller2vec_kernel(tc, x, pos, w_pos, b0, w1, b1, w2, b2, offs, out):
         b2_scaled = held.tile([P, DB], F32, name="b2_scaled")
         nc.gpsimd.tensor_scalar(b2_scaled[:], b2_sb[:], SCALE, None, MULT)
 
-        ident = held.tile([P, P], F32, name="ident")
-        make_identity(nc, ident[:])
-        for b in range(CB):
-            flipped = psum.tile([P, PIECE], F32, name="bank")
-            nc.tensor.transpose(flipped[:Q, :P], wpos_sb[:, b, :], ident[:])
-            nc.vector.tensor_copy(wposT_pad[:Q, b * P : (b + 1) * P], flipped[:Q, :P])
-
         for p in range(PIECES):
             cols = slice(p * PIECE, (p + 1) * PIECE)
             nc.vector.tensor_copy(pos_pad[:Q, cols], pos_sb[:, cols])
+
+        ident = held.tile([P, P], F32, name="ident")
+        make_identity(nc, ident[:])
+        flipped = psum.tile([P, PIECE], F32, name="bank")
+        for b in range(CB):
+            nc.tensor.transpose(flipped[:Q, b * P : (b + 1) * P], wpos_sb[:, b, :], ident[:])
+        nc.vector.tensor_copy(wposT_pad[:Q, :], flipped[:Q, :C])
 
         other_sb = [held.tile([P, N], F32, name=f"other_sb{b}") for b in range(CB)]
         h0 = [[held.tile([P, PIECE], BF16, name=f"h0_{b}_{p}") for p in range(PIECES)] for b in range(CB)]
@@ -124,13 +124,13 @@ def tile_baller2vec_kernel(tc, x, pos, w_pos, b0, w1, b1, w2, b2, offs, out):
         for p in range(PIECES):
             look_up(0, p)
             make_other(1, p)
-        layer1_block0(0)
-        layer1_block0(1)
-        for step in range(PIECES + 1):
-            if step < PIECES:
-                look_up(1, step)
-                layer1_block1(step)
-            if step + 2 < PIECES:
-                layer1_block0(step + 2)
-            if step >= 1:
-                layer2(step - 1)
+        for p in range(PIECES):
+            layer1_block0(p)
+        for p in range(PIECES):
+            look_up(1, p)
+        layer1_block1(0)
+        layer1_block1(1)
+        for p in range(PIECES):
+            layer2(p)
+            if p + 2 < PIECES:
+                layer1_block1(p + 2)

@@ -39,7 +39,8 @@ def tile_baller2vec_kernel(tc, x, pos, w_pos, b0, w1, b1, w2, b2, offs, out):
         offsets = held.tile([P, N // 16], U16, name="offsets")
         nc.sync.dma_start(offsets[:], offs)
         pos_sb = held.tile([Q, N], F32, name="pos_sb")
-        nc.sync.dma_start(pos_sb[:], pos)
+        nc.sync.dma_start(pos_sb[0:2, :], pos[0:2, :])
+        nc.sync.dma_start(pos_sb[2:3, :], pos[2:3, :])
         wpos_sb = held.tile([P, CB, Q], F32, name="wpos_sb")
         nc.sync.dma_start(wpos_sb[:], w_pos.rearrange("(b p) q -> p b q", p=P))
         b0_sb = held.tile([P, CB], F32, name="b0_sb")
@@ -87,10 +88,7 @@ def tile_baller2vec_kernel(tc, x, pos, w_pos, b0, w1, b1, w2, b2, offs, out):
             piece_offsets = offsets[:, p * (PIECE // 16) : (p + 1) * (PIECE // 16)]
             summed = work.tile([P, PIECE], F32, name="summed")
             nc.vector.tensor_tensor(summed[:], x_sb[b][:].indirect(piece_offsets), other_sb[b][:, cols], ADD)
-            if b == 0:
-                nc.scalar.activation(h0[b][p][:], summed[:], RELU)
-            else:
-                nc.vector.tensor_scalar(h0[b][p][:], summed[:], 0.0, None, MAX)
+            nc.scalar.activation(h0[b][p][:], summed[:], RELU)
 
         acc_h1 = {}
 

@@ -13,6 +13,10 @@ SCALE = math.sqrt(D)
 CB, MB, DB = C // P, M1 // P, D // P
 PIECE = 512
 PIECES = N // PIECE
+WIDTHS = (PIECE // 2, PIECE // 2, PIECE, PIECE, PIECE)
+STARTS = tuple(sum(WIDTHS[:s]) for s in range(len(WIDTHS)))
+STEPS = len(WIDTHS)
+OPEN = 4
 WARM_UP = 4
 FLOPS = 2 * N * (C * Q + C * M1 + M1 * D)
 
@@ -25,13 +29,18 @@ def tile_baller2vec_kernel(tc, x, pos, w_pos, b0, w1, b1, w2, b2, offs, out):
         tc.tile_pool(name="stage", bufs=8) as stage,
         tc.psum_pool(name="psum", bufs=8) as psum,
     ):
-        pos_pad = held.tile([P, N], F32, name="pos_pad")
-        nc.vector.memset(pos_pad[:], 0.0)
-        wposT_pad = held.tile([P, C], F32, name="wposT_pad")
-        nc.vector.memset(wposT_pad[:], 0.0)
-
         zeros = held.tile([P, PIECE], BF16, name="zeros")
         nc.gpsimd.memset(zeros[:], 0.0)
+        ident = held.tile([P, P], F32, name="ident")
+        make_identity(nc, ident[:])
+
+        wposT_pad = held.tile([P, C], F32, name="wposT_pad")
+        nc.vector.memset(wposT_pad[:], 0.0)
+        pos_pad = held.tile([P, N], F32, name="pos_pad")
+        for p in range(PIECES):
+            zero_engine = nc.vector if p < PIECES // 2 else nc.gpsimd
+            zero_engine.memset(pos_pad[:, p * PIECE : (p + 1) * PIECE], 0.0)
+
         for i in range(WARM_UP):
             unused = psum.tile([P, PIECE], F32, name="bank")
             nc.tensor.matmul(unused[:], zeros[:, :P], zeros[:], start=True, stop=True)
@@ -62,20 +71,23 @@ def tile_baller2vec_kernel(tc, x, pos, w_pos, b0, w1, b1, w2, b2, offs, out):
         b2_scaled = held.tile([P, DB], F32, name="b2_scaled")
         nc.gpsimd.tensor_scalar(b2_scaled[:], b2_sb[:], SCALE, None, MULT)
 
-        for p in range(PIECES):
+        def pad_pos(p):
             cols = slice(p * PIECE, (p + 1) * PIECE)
             nc.vector.tensor_copy(pos_pad[:Q, cols], pos_sb[:, cols])
 
-        ident = held.tile([P, P], F32, name="ident")
-        make_identity(nc, ident[:])
+        pad_pos(0)
+
         flipped = psum.tile([P, PIECE], F32, name="bank")
         for b in range(CB):
             nc.tensor.transpose(flipped[:Q, b * P : (b + 1) * P], wpos_sb[:, b, :], ident[:])
         nc.vector.tensor_copy(wposT_pad[:Q, :], flipped[:Q, :C])
 
+        for p in range(1, PIECES):
+            pad_pos(p)
+
         other_sb = [held.tile([P, N], F32, name=f"other_sb{b}") for b in range(CB)]
-        h0 = [[held.tile([P, PIECE], BF16, name=f"h0_{b}_{p}") for p in range(PIECES)] for b in range(CB)]
-        h1 = [held.tile([P, MB, PIECE], BF16, name=f"h1_{p}") for p in range(PIECES)]
+        h0 = [[held.tile([P, WIDTHS[s]], BF16, name=f"h0_{b}_{s}") for s in range(STEPS)] for b in range(CB)]
+        h1 = [held.tile([P, MB, WIDTHS[s]], BF16, name=f"h1_{s}") for s in range(STEPS)]
 
         def make_other(b, p):
             cols = slice(p * PIECE, (p + 1) * PIECE)
@@ -83,52 +95,62 @@ def tile_baller2vec_kernel(tc, x, pos, w_pos, b0, w1, b1, w2, b2, offs, out):
             nc.tensor.matmul(acc_other[:], wposT_pad[:, b * P : (b + 1) * P], pos_pad[:, cols], start=True, stop=True)
             nc.scalar.activation(other_sb[b][:, cols], acc_other[:], IDENTITY, bias=b0_sb[:, b : b + 1])
 
-        def look_up(b, p):
-            cols = slice(p * PIECE, (p + 1) * PIECE)
-            piece_offsets = offsets[:, p * (PIECE // 16) : (p + 1) * (PIECE // 16)]
+        def look_up(b, s):
+            width = WIDTHS[s]
+            cols = slice(STARTS[s], STARTS[s] + width)
+            step_offsets = offsets[:, STARTS[s] // 16 : (STARTS[s] + width) // 16]
             summed = work.tile([P, PIECE], F32, name="summed")
-            nc.vector.tensor_tensor(summed[:], x_sb[b][:].indirect(piece_offsets), other_sb[b][:, cols], ADD)
-            nc.scalar.activation(h0[b][p][:], summed[:], RELU)
+            nc.vector.tensor_tensor(summed[:, :width], x_sb[b][:].indirect(step_offsets), other_sb[b][:, cols], ADD)
+            nc.scalar.activation(h0[b][s][:], summed[:, :width], RELU)
 
         acc_h1 = {}
 
-        def layer1_block0(p):
-            acc_h1[p] = [psum.tile([P, PIECE], F32, name="bank") for m in range(MB)]
+        def layer1_block0(s):
+            acc_h1[s] = [psum.tile([P, PIECE], F32, name="bank") for m in range(MB)]
             for m in range(MB):
-                nc.tensor.matmul(acc_h1[p][m][:], w1_sb[:, 0, m * P : (m + 1) * P], h0[0][p][:], start=True, stop=False)
+                nc.tensor.matmul(
+                    acc_h1[s][m][:, : WIDTHS[s]], w1_sb[:, 0, m * P : (m + 1) * P], h0[0][s][:], start=True, stop=False
+                )
 
-        def layer1_block1(p):
+        def layer1_block1(s):
+            if s >= OPEN:
+                layer1_block0(s)
             for m in range(MB):
-                nc.tensor.matmul(acc_h1[p][m][:], w1_sb[:, 1, m * P : (m + 1) * P], h0[1][p][:], start=False, stop=True)
-                nc.scalar.activation(h1[p][:, m, :], acc_h1[p][m][:], RELU, bias=b1_sb[:, m : m + 1])
+                nc.tensor.matmul(
+                    acc_h1[s][m][:, : WIDTHS[s]], w1_sb[:, 1, m * P : (m + 1) * P], h0[1][s][:], start=False, stop=True
+                )
+                nc.scalar.activation(h1[s][:, m, :], acc_h1[s][m][:, : WIDTHS[s]], RELU, bias=b1_sb[:, m : m + 1])
 
-        def layer2(p):
-            cols = slice(p * PIECE, (p + 1) * PIECE)
+        def layer2(s):
+            width = WIDTHS[s]
+            cols = slice(STARTS[s], STARTS[s] + width)
             for d in range(DB):
                 acc_out = psum.tile([P, PIECE], F32, name="bank")
                 for m in range(MB):
                     nc.tensor.matmul(
-                        acc_out[:], w2_sb[:, m, d * P : (d + 1) * P], h1[p][:, m, :], start=(m == 0), stop=(m == MB - 1)
+                        acc_out[:, :width], w2_sb[:, m, d * P : (d + 1) * P], h1[s][:, m, :], start=(m == 0), stop=(m == MB - 1)
                     )
                 staged = stage.tile([P, PIECE], F32, name="staged")
                 if d % 2 == 0:
-                    nc.scalar.activation(staged[:], acc_out[:], IDENTITY, bias=b2_scaled[:, d : d + 1], scale=SCALE)
+                    nc.scalar.activation(
+                        staged[:, :width], acc_out[:, :width], IDENTITY, bias=b2_scaled[:, d : d + 1], scale=SCALE
+                    )
                 else:
-                    nc.vector.tensor_scalar(staged[:], acc_out[:], SCALE, b2_scaled[:, d : d + 1], MULT, ADD)
-                nc.sync.dma_start(out[d * P : (d + 1) * P, cols], staged[:])
+                    nc.vector.tensor_scalar(staged[:, :width], acc_out[:, :width], SCALE, b2_scaled[:, d : d + 1], MULT, ADD)
+                nc.sync.dma_start(out[d * P : (d + 1) * P, cols], staged[:, :width])
 
         for p in range(PIECES):
             make_other(0, p)
+        look_up(0, 0)
         for p in range(PIECES):
-            look_up(0, p)
+            look_up(0, p + 1)
             make_other(1, p)
-        for p in range(PIECES):
-            layer1_block0(p)
-        for p in range(PIECES):
-            look_up(1, p)
-        layer1_block1(0)
-        layer1_block1(1)
-        for p in range(PIECES):
-            layer2(p)
-            if p + 2 < PIECES:
-                layer1_block1(p + 2)
+        for s in range(OPEN):
+            layer1_block0(s)
+        for t in range(STEPS + 2):
+            if t < STEPS:
+                look_up(1, t)
+            if 1 <= t <= STEPS:
+                layer1_block1(t - 1)
+            if t >= 2:
+                layer2(t - 2)

@@ -45,23 +45,24 @@ def tile_baller2vec_kernel(tc, x, pos, w_pos, b0, w1, b1, w2, b2, offs, out):
             unused = psum.tile([P, PIECE], F32, name="bank")
             nc.tensor.matmul(unused[:], zeros[:, :P], zeros[:], start=True, stop=True)
 
+        x_blocks = x.rearrange("(p b) s -> b p s", b=CB)
         offsets = held.tile([P, N // 16], U16, name="offsets")
         nc.sync.dma_start(offsets[:], offs)
         pos_sb = held.tile([Q, N], F32, name="pos_sb")
         nc.sync.dma_start(pos_sb[0:2, :], pos[0:2, :])
         nc.sync.dma_start(pos_sb[2:3, :], pos[2:3, :])
         wpos_sb = held.tile([P, CB, Q], F32, name="wpos_sb")
-        nc.sync.dma_start(wpos_sb[:], w_pos.rearrange("(b p) q -> p b q", p=P))
+        nc.sync.dma_start(wpos_sb[:], w_pos.rearrange("(p b) q -> p b q", b=CB))
         b0_sb = held.tile([P, CB], F32, name="b0_sb")
         b1_sb = held.tile([P, MB], F32, name="b1_sb")
         b2_sb = held.tile([P, DB], F32, name="b2_sb")
         with nc.allow_non_contiguous_dma(reason="a bias: one element to a partition"):
-            nc.sync.dma_start(b0_sb[:], b0.rearrange("(b p) o -> p (b o)", p=P))
+            nc.sync.dma_start(b0_sb[:], b0.rearrange("(p b) o -> p (b o)", b=CB))
         x_sb = [held.tile([P, S], F32, name=f"x_sb{b}") for b in range(CB)]
-        nc.sync.dma_start(x_sb[0][:], x[0:P, :])
+        nc.sync.dma_start(x_sb[0][:], x_blocks[0, :, :])
         w1_sb = held.tile([P, CB, M1], BF16, name="w1_sb")
-        nc.sync.dma_start(w1_sb[:], w1.rearrange("(b p) m -> p b m", p=P))
-        nc.sync.dma_start(x_sb[1][:], x[P : 2 * P, :])
+        nc.sync.dma_start(w1_sb[:], w1.rearrange("(p b) m -> p b m", b=CB))
+        nc.sync.dma_start(x_sb[1][:], x_blocks[1, :, :])
         w2_sb = held.tile([P, MB, D], BF16, name="w2_sb")
         nc.sync.dma_start(w2_sb[:], w2.rearrange("(b p) d -> p b d", p=P))
         with nc.allow_non_contiguous_dma(reason="a bias: one element to a partition"):

@@ -26,7 +26,7 @@ def tile_baller2vec_kernel(tc, x, pos, w_pos, b0, w1, b1, w2, b2, offs, out):
     with (
         tc.tile_pool(name="held", bufs=1) as held,
         tc.tile_pool(name="work", bufs=4) as work,
-        tc.tile_pool(name="stage", bufs=8) as stage,
+        tc.tile_pool(name="stage", bufs=20) as stage,
         tc.psum_pool(name="psum", bufs=8) as psum,
     ):
         zeros = held.tile([P, PIECE], BF16, name="zeros")

@@ -4,7 +4,7 @@ import concourse.mybir as mybir
 from concourse.masks import make_identity
 
 F32, BF16, U16 = mybir.dt.float32, mybir.dt.bfloat16, mybir.dt.uint16
-ADD, MULT, MAX = mybir.AluOpType.add, mybir.AluOpType.mult, mybir.AluOpType.max
+ADD, SUB, MULT, MAX = mybir.AluOpType.add, mybir.AluOpType.subtract, mybir.AluOpType.mult, mybir.AluOpType.max
 IDENTITY, RELU = mybir.ActivationFunctionType.Identity, mybir.ActivationFunctionType.Relu
 
 P = 128
@@ -13,11 +13,15 @@ SCALE = math.sqrt(D)
 CB, MB, DB = C // P, M1 // P, D // P
 PIECE = 512
 PIECES = N // PIECE
+CHUNKS = N // P
+PARTS = 3
+ROWS = PARTS * PARTS * Q
+POS_ROWS = 64
 WIDTHS = (PIECE // 2, PIECE // 2, PIECE, PIECE, PIECE)
 STARTS = tuple(sum(WIDTHS[:s]) for s in range(len(WIDTHS)))
 STEPS = len(WIDTHS)
 OPEN = 4
-WARM_UP = 4
+WARM_UP = 3
 FLOPS = 2 * N * (C * Q + C * M1 + M1 * D)
 
 
@@ -25,34 +29,37 @@ def tile_baller2vec_kernel(tc, x, pos, w_pos, b0, w1, b1, w2, b2, offs, out):
     nc = tc.nc
     with (
         tc.tile_pool(name="held", bufs=1) as held,
-        tc.tile_pool(name="work", bufs=4) as work,
+        tc.tile_pool(name="work", bufs=5) as work,
+        tc.tile_pool(name="ring", bufs=2) as ring,
         tc.tile_pool(name="stage", bufs=20) as stage,
         tc.psum_pool(name="psum", bufs=8) as psum,
     ):
         zeros = held.tile([P, PIECE], BF16, name="zeros")
         nc.gpsimd.memset(zeros[:], 0.0)
-        ident = held.tile([P, P], F32, name="ident")
+        ident = held.tile([P, P], BF16, name="ident")
         make_identity(nc, ident[:])
 
-        wposT_pad = held.tile([P, C], F32, name="wposT_pad")
-        nc.vector.memset(wposT_pad[:], 0.0)
-        pos_pad = held.tile([P, N], F32, name="pos_pad")
-        for p in range(PIECES):
-            zero_engine = nc.vector if p < PIECES // 2 else nc.gpsimd
-            zero_engine.memset(pos_pad[:, p * PIECE : (p + 1) * PIECE], 0.0)
+        pos_parts = held.tile([P, CHUNKS, P], BF16, name="pos_parts")
+        nc.vector.memset(pos_parts[:], 0.0)
+        w_parts = held.tile([P, CB, P], BF16, name="w_parts")
+        nc.gpsimd.memset(w_parts[:], 0.0)
+        ident_f32 = held.tile([POS_ROWS, POS_ROWS], F32, name="ident_f32")
+        nc.vector.tensor_copy(ident_f32[:], ident[:POS_ROWS, :POS_ROWS])
 
         for i in range(WARM_UP):
             unused = psum.tile([P, PIECE], F32, name="bank")
             nc.tensor.matmul(unused[:], zeros[:, :P], zeros[:], start=True, stop=True)
 
         x_blocks = x.rearrange("(p b) s -> b p s", b=CB)
-        offsets = held.tile([P, N // 16], U16, name="offsets")
-        nc.sync.dma_start(offsets[:], offs)
-        pos_sb = held.tile([Q, N], F32, name="pos_sb")
-        nc.sync.dma_start(pos_sb[0:2, :], pos[0:2, :])
-        nc.sync.dma_start(pos_sb[2:3, :], pos[2:3, :])
+        pos_sb = held.tile([POS_ROWS, P], F32, name="pos_sb")
+        pos_rows = pos.rearrange("q (k t) -> (q k) t", t=P)
+        nc.sync.dma_start(pos_sb[0:32, :], pos_rows[0:32, :])
+        nc.sync.dma_start(pos_sb[32:48, :], pos_rows[32:48, :])
+        nc.sync.dma_start(pos_sb[48:64, :], pos_rows[32:48, :])
         wpos_sb = held.tile([P, CB, Q], F32, name="wpos_sb")
         nc.sync.dma_start(wpos_sb[:], w_pos.rearrange("(p b) q -> p b q", b=CB))
+        offsets = held.tile([P, N // 16], U16, name="offsets")
+        nc.sync.dma_start(offsets[:], offs)
         b0_sb = held.tile([P, CB], F32, name="b0_sb")
         b1_sb = held.tile([P, MB], F32, name="b1_sb")
         b2_sb = held.tile([P, DB], F32, name="b2_sb")
@@ -69,40 +76,86 @@ def tile_baller2vec_kernel(tc, x, pos, w_pos, b0, w1, b1, w2, b2, offs, out):
             nc.sync.dma_start(b1_sb[:], b1.rearrange("(b p) o -> p (b o)", p=P))
             nc.sync.dma_start(b2_sb[:], b2.rearrange("(b p) o -> p (b o)", p=P))
 
+        w_cols = w_parts[:, :, :ROWS].rearrange("p k (a b q) -> p k a b q", a=PARTS, b=PARTS)
+        w_rest = held.tile([P, CB, Q], F32, name="w_rest")
+
+        def to_all_a(ap):
+            return ap.unsqueeze(2).to_broadcast([P, CB, PARTS, Q])
+
+        nc.gpsimd.tensor_copy(w_cols[:, :, :, 0, :], to_all_a(wpos_sb[:]))
+        nc.gpsimd.tensor_tensor(w_cols[:, :, :, 1, :], to_all_a(wpos_sb[:]), w_cols[:, :, :, 0, :], SUB)
+        nc.gpsimd.tensor_tensor(w_rest[:], wpos_sb[:], w_cols[:, :, 0, 0, :], SUB)
+        nc.gpsimd.tensor_tensor(w_cols[:, :, :, 2, :], to_all_a(w_rest[:]), w_cols[:, :, :, 1, :], SUB)
+
+        flipped_pos = psum.tile([P, PIECE], F32, name="bank")
+        nc.tensor.transpose(flipped_pos[:, :POS_ROWS], pos_sb[:], ident_f32[:])
+        pos_tok = flipped_pos[:, : Q * CHUNKS].rearrange("p (q k) -> p k q", q=Q)
+        p_cols = pos_parts[:, :, :ROWS].rearrange("p k (a b q) -> p k a b q", a=PARTS, b=PARTS)
+        p_rest = held.tile([P, CHUNKS, Q], F32, name="p_rest")
+
+        def split_pos(chunks):
+            def to_all_b(ap):
+                return ap.unsqueeze(2).to_broadcast([P, chunks.stop - chunks.start, PARTS, Q])
+
+            tok, rest, cols = pos_tok[:, chunks, :], p_rest[:, chunks, :], p_cols[:, chunks, :, :, :]
+            nc.vector.tensor_copy(cols[:, :, 0, :, :], to_all_b(tok))
+            nc.vector.tensor_tensor(cols[:, :, 1, :, :], to_all_b(tok), cols[:, :, 0, :, :], SUB)
+            nc.vector.tensor_tensor(rest, tok, cols[:, :, 0, 0, :], SUB)
+            nc.vector.tensor_tensor(cols[:, :, 2, :, :], to_all_b(rest), cols[:, :, 1, :, :], SUB)
+
+        w_rows = held.tile([P, C], BF16, name="w_rows")
+        flipped_w = psum.tile([P, 2 * PIECE], BF16, name="bank")
+        for b in range(CB):
+            nc.tensor.transpose(flipped_w[:, b * P : (b + 1) * P], w_parts[:, b, :], ident[:])
+        nc.scalar.copy(w_rows[:], flipped_w[:, :C])
+
+        p_rows = held.tile([P, N], BF16, name="p_rows")
+        first_piece = slice(0, PIECE // P)
+        split_pos(first_piece)
+
+        def flip_pos(p):
+            flipped = psum.tile([P, 2 * PIECE], BF16, name="bank")
+            for k in range(PIECE // P):
+                nc.tensor.transpose(flipped[:, k * P : (k + 1) * P], pos_parts[:, p * (PIECE // P) + k, :], ident[:])
+            if p == 0:
+                nc.scalar.copy(p_rows[:, :PIECE], flipped[:, :PIECE])
+            else:
+                nc.vector.tensor_copy(p_rows[:, p * PIECE : (p + 1) * PIECE], flipped[:, :PIECE])
+
+        flip_pos(0)
+        split_pos(slice(PIECE // P, CHUNKS))
+        for p in range(1, PIECES):
+            flip_pos(p)
+
         b2_scaled = held.tile([P, DB], F32, name="b2_scaled")
         nc.gpsimd.tensor_scalar(b2_scaled[:], b2_sb[:], SCALE, None, MULT)
 
-        def pad_pos(p):
-            cols = slice(p * PIECE, (p + 1) * PIECE)
-            nc.vector.tensor_copy(pos_pad[:Q, cols], pos_sb[:, cols])
-
-        pad_pos(0)
-
-        flipped = psum.tile([P, PIECE], F32, name="bank")
-        for b in range(CB):
-            nc.tensor.transpose(flipped[:Q, b * P : (b + 1) * P], wpos_sb[:, b, :], ident[:])
-        nc.vector.tensor_copy(wposT_pad[:Q, :], flipped[:Q, :C])
-
-        for p in range(1, PIECES):
-            pad_pos(p)
-
         other_sb = [held.tile([P, N], F32, name=f"other_sb{b}") for b in range(CB)]
-        h0 = [[held.tile([P, WIDTHS[s]], BF16, name=f"h0_{b}_{s}") for s in range(STEPS)] for b in range(CB)]
+        h0 = {}
         h1 = [held.tile([P, MB, WIDTHS[s]], BF16, name=f"h1_{s}") for s in range(STEPS)]
 
-        def make_other(b, p):
-            cols = slice(p * PIECE, (p + 1) * PIECE)
+        def make_other(b, s):
+            width = WIDTHS[s]
+            cols = slice(STARTS[s], STARTS[s] + width)
             acc_other = psum.tile([P, PIECE], F32, name="bank")
-            nc.tensor.matmul(acc_other[:], wposT_pad[:, b * P : (b + 1) * P], pos_pad[:, cols], start=True, stop=True)
-            nc.scalar.activation(other_sb[b][:, cols], acc_other[:], IDENTITY, bias=b0_sb[:, b : b + 1])
+            nc.tensor.matmul(acc_other[:, :width], w_rows[:, b * P : (b + 1) * P], p_rows[:, cols], start=True, stop=True)
+            nc.scalar.activation(other_sb[b][:, cols], acc_other[:, :width], IDENTITY, bias=b0_sb[:, b : b + 1])
+
+        summed = {}
 
         def look_up(b, s):
             width = WIDTHS[s]
             cols = slice(STARTS[s], STARTS[s] + width)
             step_offsets = offsets[:, STARTS[s] // 16 : (STARTS[s] + width) // 16]
-            summed = work.tile([P, PIECE], F32, name="summed")
-            nc.vector.tensor_tensor(summed[:, :width], x_sb[b][:].indirect(step_offsets), other_sb[b][:, cols], ADD)
-            nc.scalar.activation(h0[b][s][:], summed[:, :width], RELU)
+            summed[b, s] = (work if b == 0 else ring).tile([P, PIECE], F32, name=f"summed{b}")
+            nc.vector.tensor_tensor(summed[b, s][:, :width], x_sb[b][:].indirect(step_offsets), other_sb[b][:, cols], ADD)
+
+        def relu_h0(b, s):
+            h0[b, s] = (work if b == 0 else ring).tile([P, PIECE], BF16, name=f"h0_{b}")
+            if b == 0 or s < 2:
+                nc.scalar.activation(h0[b, s][:, : WIDTHS[s]], summed[b, s][:, : WIDTHS[s]], RELU)
+            else:
+                nc.vector.tensor_scalar(h0[b, s][:, : WIDTHS[s]], summed[b, s][:, : WIDTHS[s]], 0.0, None, MAX)
 
         acc_h1 = {}
 
@@ -110,7 +163,7 @@ def tile_baller2vec_kernel(tc, x, pos, w_pos, b0, w1, b1, w2, b2, offs, out):
             acc_h1[s] = [psum.tile([P, PIECE], F32, name="bank") for m in range(MB)]
             for m in range(MB):
                 nc.tensor.matmul(
-                    acc_h1[s][m][:, : WIDTHS[s]], w1_sb[:, 0, m * P : (m + 1) * P], h0[0][s][:], start=True, stop=False
+                    acc_h1[s][m][:, : WIDTHS[s]], w1_sb[:, 0, m * P : (m + 1) * P], h0[0, s][:, : WIDTHS[s]], start=True, stop=False
                 )
 
         def layer1_block1(s):
@@ -118,7 +171,7 @@ def tile_baller2vec_kernel(tc, x, pos, w_pos, b0, w1, b1, w2, b2, offs, out):
                 layer1_block0(s)
             for m in range(MB):
                 nc.tensor.matmul(
-                    acc_h1[s][m][:, : WIDTHS[s]], w1_sb[:, 1, m * P : (m + 1) * P], h0[1][s][:], start=False, stop=True
+                    acc_h1[s][m][:, : WIDTHS[s]], w1_sb[:, 1, m * P : (m + 1) * P], h0[1, s][:, : WIDTHS[s]], start=False, stop=True
                 )
                 nc.scalar.activation(h1[s][:, m, :], acc_h1[s][m][:, : WIDTHS[s]], RELU, bias=b1_sb[:, m : m + 1])
 
@@ -132,7 +185,7 @@ def tile_baller2vec_kernel(tc, x, pos, w_pos, b0, w1, b1, w2, b2, offs, out):
                         acc_out[:, :width], w2_sb[:, m, d * P : (d + 1) * P], h1[s][:, m, :], start=(m == 0), stop=(m == MB - 1)
                     )
                 staged = stage.tile([P, PIECE], F32, name="staged")
-                if d % 2 == 0:
+                if s < 2 or (s * DB + d) % 3 == 0:
                     nc.scalar.activation(
                         staged[:, :width], acc_out[:, :width], IDENTITY, bias=b2_scaled[:, d : d + 1], scale=SCALE
                     )
@@ -140,17 +193,22 @@ def tile_baller2vec_kernel(tc, x, pos, w_pos, b0, w1, b1, w2, b2, offs, out):
                     nc.vector.tensor_scalar(staged[:, :width], acc_out[:, :width], SCALE, b2_scaled[:, d : d + 1], MULT, ADD)
                 nc.sync.dma_start(out[d * P : (d + 1) * P, cols], staged[:, :width])
 
-        for p in range(PIECES):
-            make_other(0, p)
-        look_up(0, 0)
-        for p in range(PIECES):
-            look_up(0, p + 1)
-            make_other(1, p)
+        for s in range(STEPS):
+            make_other(0, s)
+        for s in range(STEPS):
+            look_up(0, s)
+            if s < OPEN:
+                relu_h0(0, s)
+            make_other(1, s)
         for s in range(OPEN):
             layer1_block0(s)
         for t in range(STEPS + 2):
             if t < STEPS:
                 look_up(1, t)
+                relu_h0(1, t)
+            if t == 1:
+                for s in range(OPEN, STEPS):
+                    relu_h0(0, s)
             if 1 <= t <= STEPS:
                 layer1_block1(t - 1)
             if t >= 2:

@@ -31,6 +31,7 @@ def tile_baller2vec_kernel(tc, x, pos, w_pos, b0, w1, b1, w2, b2, offs, out):
         tc.tile_pool(name="held", bufs=1) as held,
         tc.tile_pool(name="work", bufs=5) as work,
         tc.tile_pool(name="ring", bufs=2) as ring,
+        tc.tile_pool(name="ring_other", bufs=4) as ring_other,
         tc.tile_pool(name="stage", bufs=20) as stage,
         tc.psum_pool(name="psum", bufs=8) as psum,
     ):
@@ -130,7 +131,7 @@ def tile_baller2vec_kernel(tc, x, pos, w_pos, b0, w1, b1, w2, b2, offs, out):
         b2_scaled = held.tile([P, DB], F32, name="b2_scaled")
         nc.gpsimd.tensor_scalar(b2_scaled[:], b2_sb[:], SCALE, None, MULT)
 
-        other_sb = [held.tile([P, N], F32, name=f"other_sb{b}") for b in range(CB)]
+        other_sb = {}
         h0 = {}
         h1 = [held.tile([P, MB, WIDTHS[s]], BF16, name=f"h1_{s}") for s in range(STEPS)]
 
@@ -139,20 +140,25 @@ def tile_baller2vec_kernel(tc, x, pos, w_pos, b0, w1, b1, w2, b2, offs, out):
             cols = slice(STARTS[s], STARTS[s] + width)
             acc_other = psum.tile([P, PIECE], F32, name="bank")
             nc.tensor.matmul(acc_other[:, :width], w_rows[:, b * P : (b + 1) * P], p_rows[:, cols], start=True, stop=True)
-            nc.scalar.activation(other_sb[b][:, cols], acc_other[:, :width], IDENTITY, bias=b0_sb[:, b : b + 1])
+            other_sb[b, s] = (work if b == 0 else ring_other).tile([P, PIECE], F32, name=f"other{b}")
+            nc.scalar.activation(other_sb[b, s][:, :width], acc_other[:, :width], IDENTITY, bias=b0_sb[:, b : b + 1])
 
         summed = {}
 
         def look_up(b, s):
             width = WIDTHS[s]
-            cols = slice(STARTS[s], STARTS[s] + width)
             step_offsets = offsets[:, STARTS[s] // 16 : (STARTS[s] + width) // 16]
-            summed[b, s] = (work if b == 0 else ring).tile([P, PIECE], F32, name=f"summed{b}")
-            nc.vector.tensor_tensor(summed[b, s][:, :width], x_sb[b][:].indirect(step_offsets), other_sb[b][:, cols], ADD)
+            if b == 0:
+                summed[b, s] = work.tile([P, PIECE], F32, name="summed0")
+            elif s < 2:
+                summed[b, s] = ring.tile([P, PIECE], F32, name="summed1_early")
+            else:
+                summed[b, s] = held.tile([P, PIECE], F32, name="summed1_late")
+            nc.vector.tensor_tensor(summed[b, s][:, :width], x_sb[b][:].indirect(step_offsets), other_sb[b, s][:, :width], ADD)
 
         def relu_h0(b, s):
             h0[b, s] = (work if b == 0 else ring).tile([P, PIECE], BF16, name=f"h0_{b}")
-            if b == 0 or s < 2:
+            if (s < OPEN) if b == 0 else (s < 2):
                 nc.scalar.activation(h0[b, s][:, : WIDTHS[s]], summed[b, s][:, : WIDTHS[s]], RELU)
             else:
                 nc.vector.tensor_scalar(h0[b, s][:, : WIDTHS[s]], summed[b, s][:, : WIDTHS[s]], 0.0, None, MAX)
@@ -199,7 +205,7 @@ def tile_baller2vec_kernel(tc, x, pos, w_pos, b0, w1, b1, w2, b2, offs, out):
             look_up(0, s)
             if s < OPEN:
                 relu_h0(0, s)
-            make_other(1, s)
+                make_other(1, s)
         for s in range(OPEN):
             layer1_block0(s)
         for t in range(STEPS + 2):
@@ -208,6 +214,7 @@ def tile_baller2vec_kernel(tc, x, pos, w_pos, b0, w1, b1, w2, b2, offs, out):
                 relu_h0(1, t)
             if t == 1:
                 for s in range(OPEN, STEPS):
+                    make_other(1, s)
                     relu_h0(0, s)
             if 1 <= t <= STEPS:
                 layer1_block1(t - 1)

@@ -17,9 +17,12 @@ CHUNKS = N // P
 PARTS = 3
 ROWS = PARTS * PARTS * Q
 POS_ROWS = 64
-WIDTHS = (PIECE // 2, PIECE // 2, PIECE, PIECE, PIECE)
+WIDTHS = (PIECE // 2, PIECE // 2, PIECE, PIECE, PIECE // 2, PIECE // 2)
 STARTS = tuple(sum(WIDTHS[:s]) for s in range(len(WIDTHS)))
 STEPS = len(WIDTHS)
+PARTS_0 = (PIECE // 2, PIECE // 2, PIECE, PIECE, PIECE)
+STARTS_0 = tuple(sum(PARTS_0[:i]) for i in range(len(PARTS_0)))
+LAST_0 = len(PARTS_0) - 1
 OPEN = 4
 WARM_UP = 3
 FLOPS = 2 * N * (C * Q + C * M1 + M1 * D)
@@ -29,10 +32,10 @@ def tile_baller2vec_kernel(tc, x, pos, w_pos, b0, w1, b1, w2, b2, offs, out):
     nc = tc.nc
     with (
         tc.tile_pool(name="held", bufs=1) as held,
-        tc.tile_pool(name="work", bufs=5) as work,
+        tc.tile_pool(name="work", bufs=6) as work,
         tc.tile_pool(name="ring", bufs=2) as ring,
         tc.tile_pool(name="ring_other", bufs=4) as ring_other,
-        tc.tile_pool(name="stage", bufs=20) as stage,
+        tc.tile_pool(name="stage", bufs=24) as stage,
         tc.psum_pool(name="psum", bufs=8) as psum,
     ):
         zeros = held.tile([P, PIECE], BF16, name="zeros")
@@ -135,41 +138,47 @@ def tile_baller2vec_kernel(tc, x, pos, w_pos, b0, w1, b1, w2, b2, offs, out):
         h0 = {}
         h1 = [held.tile([P, MB, WIDTHS[s]], BF16, name=f"h1_{s}") for s in range(STEPS)]
 
-        def make_other(b, s):
-            width = WIDTHS[s]
-            cols = slice(STARTS[s], STARTS[s] + width)
+        def make_other(b, i):
+            width = PARTS_0[i]
+            cols = slice(STARTS_0[i], STARTS_0[i] + width)
             acc_other = psum.tile([P, PIECE], F32, name="bank")
             nc.tensor.matmul(acc_other[:, :width], w_rows[:, b * P : (b + 1) * P], p_rows[:, cols], start=True, stop=True)
-            other_sb[b, s] = (work if b == 0 else ring_other).tile([P, PIECE], F32, name=f"other{b}")
-            nc.scalar.activation(other_sb[b, s][:, :width], acc_other[:, :width], IDENTITY, bias=b0_sb[:, b : b + 1])
+            other_sb[b, i] = (work if b == 0 else ring_other).tile([P, PIECE], F32, name=f"other{b}")
+            nc.scalar.activation(other_sb[b, i][:, :width], acc_other[:, :width], IDENTITY, bias=b0_sb[:, b : b + 1])
 
         summed = {}
 
         def look_up(b, s):
-            width = WIDTHS[s]
-            step_offsets = offsets[:, STARTS[s] // 16 : (STARTS[s] + width) // 16]
+            width = PARTS_0[s] if b == 0 else WIDTHS[s]
+            start = STARTS_0[s] if b == 0 else STARTS[s]
+            step_offsets = offsets[:, start // 16 : (start + width) // 16]
+            i = min(s, LAST_0)
+            within = slice(start - STARTS_0[i], start - STARTS_0[i] + width)
             if b == 0:
                 summed[b, s] = work.tile([P, PIECE], F32, name="summed0")
-            elif s < 2:
-                summed[b, s] = ring.tile([P, PIECE], F32, name="summed1_early")
+            elif WIDTHS[s] < PIECE:
+                summed[b, s] = held.tile([P, PIECE], F32, name=f"summed1_{s}")
             else:
-                summed[b, s] = held.tile([P, PIECE], F32, name="summed1_late")
-            nc.vector.tensor_tensor(summed[b, s][:, :width], x_sb[b][:].indirect(step_offsets), other_sb[b, s][:, :width], ADD)
+                summed[b, s] = held.tile([P, PIECE], F32, name="summed1_full")
+            nc.vector.tensor_tensor(summed[b, s][:, :width], x_sb[b][:].indirect(step_offsets), other_sb[b, i][:, within], ADD)
 
         def relu_h0(b, s):
             h0[b, s] = (work if b == 0 else ring).tile([P, PIECE], BF16, name=f"h0_{b}")
-            if (s < OPEN) if b == 0 else (s < 2):
-                nc.scalar.activation(h0[b, s][:, : WIDTHS[s]], summed[b, s][:, : WIDTHS[s]], RELU)
+            width = PARTS_0[s] if b == 0 else WIDTHS[s]
+            if (s < OPEN) if b == 0 else (WIDTHS[s] < PIECE):
+                nc.scalar.activation(h0[b, s][:, :width], summed[b, s][:, :width], RELU)
             else:
-                nc.vector.tensor_scalar(h0[b, s][:, : WIDTHS[s]], summed[b, s][:, : WIDTHS[s]], 0.0, None, MAX)
+                nc.vector.tensor_scalar(h0[b, s][:, :width], summed[b, s][:, :width], 0.0, None, MAX)
 
         acc_h1 = {}
 
         def layer1_block0(s):
             acc_h1[s] = [psum.tile([P, PIECE], F32, name="bank") for m in range(MB)]
+            i = min(s, LAST_0)
+            within = slice(STARTS[s] - STARTS_0[i], STARTS[s] - STARTS_0[i] + WIDTHS[s])
             for m in range(MB):
                 nc.tensor.matmul(
-                    acc_h1[s][m][:, : WIDTHS[s]], w1_sb[:, 0, m * P : (m + 1) * P], h0[0, s][:, : WIDTHS[s]], start=True, stop=False
+                    acc_h1[s][m][:, : WIDTHS[s]], w1_sb[:, 0, m * P : (m + 1) * P], h0[0, i][:, within], start=True, stop=False
                 )
 
         def layer1_block1(s):
@@ -199,9 +208,9 @@ def tile_baller2vec_kernel(tc, x, pos, w_pos, b0, w1, b1, w2, b2, offs, out):
                     nc.vector.tensor_scalar(staged[:, :width], acc_out[:, :width], SCALE, b2_scaled[:, d : d + 1], MULT, ADD)
                 nc.sync.dma_start(out[d * P : (d + 1) * P, cols], staged[:, :width])
 
-        for s in range(STEPS):
-            make_other(0, s)
-        for s in range(STEPS):
+        for i in range(LAST_0 + 1):
+            make_other(0, i)
+        for s in range(LAST_0 + 1):
             look_up(0, s)
             if s < OPEN:
                 relu_h0(0, s)
@@ -212,11 +221,11 @@ def tile_baller2vec_kernel(tc, x, pos, w_pos, b0, w1, b1, w2, b2, offs, out):
             if t < STEPS:
                 look_up(1, t)
                 relu_h0(1, t)
-            if t == 1:
-                for s in range(OPEN, STEPS):
-                    make_other(1, s)
-                    relu_h0(0, s)
             if 1 <= t <= STEPS:
                 layer1_block1(t - 1)
+            if t == 2:
+                for i in range(OPEN, LAST_0 + 1):
+                    make_other(1, i)
+                    relu_h0(0, i)
             if t >= 2:
                 layer2(t - 2)

@@ -24,7 +24,6 @@ PARTS_0 = (PIECE // 2, PIECE // 2, PIECE, PIECE, PIECE)
 STARTS_0 = tuple(sum(PARTS_0[:i]) for i in range(len(PARTS_0)))
 LAST_0 = len(PARTS_0) - 1
 OPEN = 4
-WARM_UP = 3
 FLOPS = 2 * N * (C * Q + C * M1 + M1 * D)
 
 
@@ -38,8 +37,6 @@ def tile_baller2vec_kernel(tc, x, pos, w_pos, b0, w1, b1, w2, b2, offs, out):
         tc.tile_pool(name="stage", bufs=24) as stage,
         tc.psum_pool(name="psum", bufs=8) as psum,
     ):
-        zeros = held.tile([P, PIECE], BF16, name="zeros")
-        nc.gpsimd.memset(zeros[:], 0.0)
         ident = held.tile([P, P], BF16, name="ident")
         make_identity(nc, ident[:])
 
@@ -49,10 +46,6 @@ def tile_baller2vec_kernel(tc, x, pos, w_pos, b0, w1, b1, w2, b2, offs, out):
         nc.gpsimd.memset(w_parts[:], 0.0)
         ident_f32 = held.tile([POS_ROWS, POS_ROWS], F32, name="ident_f32")
         nc.vector.tensor_copy(ident_f32[:], ident[:POS_ROWS, :POS_ROWS])
-
-        for i in range(WARM_UP):
-            unused = psum.tile([P, PIECE], F32, name="bank")
-            nc.tensor.matmul(unused[:], zeros[:, :P], zeros[:], start=True, stop=True)
 
         x_blocks = x.rearrange("(p b) s -> b p s", b=CB)
         pos_sb = held.tile([POS_ROWS, P], F32, name="pos_sb")

@@ -67,11 +67,11 @@ def tile_baller2vec_kernel(tc, x, pos, w_pos, b0, w1, b1, w2, b2, offs, out):
         w1_sb = held.tile([P, CB, M1], BF16, name="w1_sb")
         nc.sync.dma_start(w1_sb[:], w1.rearrange("(p b) m -> p b m", b=CB))
         nc.sync.dma_start(x_sb[1][:], x_blocks[1, :, :])
-        w2_sb = held.tile([P, MB, D], BF16, name="w2_sb")
-        nc.sync.dma_start(w2_sb[:], w2.rearrange("(b p) d -> p b d", p=P))
         with nc.allow_non_contiguous_dma(reason="a bias: one element to a partition"):
             nc.sync.dma_start(b1_sb[:], b1.rearrange("(b p) o -> p (b o)", p=P))
             nc.sync.dma_start(b2_sb[:], b2.rearrange("(b p) o -> p (b o)", p=P))
+        w2_sb = held.tile([P, MB, D], BF16, name="w2_sb")
+        nc.sync.dma_start(w2_sb[:], w2.rearrange("(b p) d -> p b d", p=P))
 
         w_cols = w_parts[:, :, :ROWS].rearrange("p k (a b q) -> p k a b q", a=PARTS, b=PARTS)
         w_rest = held.tile([P, CB, Q], F32, name="w_rest")

@@ -34,7 +34,7 @@ def tile_baller2vec_kernel(tc, x, pos, w_pos, b0, w1, b1, w2, b2, offs, out):
         tc.tile_pool(name="work", bufs=6) as work,
         tc.tile_pool(name="ring", bufs=2) as ring,
         tc.tile_pool(name="ring_other", bufs=4) as ring_other,
-        tc.tile_pool(name="stage", bufs=24) as stage,
+        tc.tile_pool(name="stage", bufs=16) as stage,
         tc.psum_pool(name="psum", bufs=8) as psum,
     ):
         ident = held.tile([P, P], BF16, name="ident")
@@ -186,20 +186,30 @@ def tile_baller2vec_kernel(tc, x, pos, w_pos, b0, w1, b1, w2, b2, offs, out):
         def layer2(s):
             width = WIDTHS[s]
             cols = slice(STARTS[s], STARTS[s] + width)
-            for d in range(DB):
-                acc_out = psum.tile([P, PIECE], F32, name="bank")
-                for m in range(MB):
-                    nc.tensor.matmul(
-                        acc_out[:, :width], w2_sb[:, m, d * P : (d + 1) * P], h1[s][:, m, :], start=(m == 0), stop=(m == MB - 1)
-                    )
-                staged = stage.tile([P, PIECE], F32, name="staged")
-                if s < 2 or (s * DB + d) % 3 == 0:
-                    nc.scalar.activation(
-                        staged[:, :width], acc_out[:, :width], IDENTITY, bias=b2_scaled[:, d : d + 1], scale=SCALE
-                    )
-                else:
-                    nc.vector.tensor_scalar(staged[:, :width], acc_out[:, :width], SCALE, b2_scaled[:, d : d + 1], MULT, ADD)
-                nc.sync.dma_start(out[d * P : (d + 1) * P, cols], staged[:, :width])
+            together = 2 if s >= OPEN else 1
+            for first in range(0, DB, together):
+                staged = stage.tile([P, together, width], F32, name=f"staged{together}")
+                for k in range(together):
+                    d = first + k
+                    acc_out = psum.tile([P, PIECE], F32, name="bank")
+                    for m in range(MB):
+                        nc.tensor.matmul(
+                            acc_out[:, :width],
+                            w2_sb[:, m, d * P : (d + 1) * P],
+                            h1[s][:, m, :],
+                            start=(m == 0),
+                            stop=(m == MB - 1),
+                        )
+                    if s < 2 or (s * DB + d) % 3 == 0:
+                        nc.scalar.activation(
+                            staged[:, k, :], acc_out[:, :width], IDENTITY, bias=b2_scaled[:, d : d + 1], scale=SCALE
+                        )
+                    else:
+                        nc.vector.tensor_scalar(
+                            staged[:, k, :], acc_out[:, :width], SCALE, b2_scaled[:, d : d + 1], MULT, ADD
+                        )
+                rows = out[first * P : (first + together) * P, cols]
+                nc.sync.dma_start(rows.rearrange("(k p) n -> p k n", p=P), staged[:])
 
         for i in range(LAST_0 + 1):
             make_other(0, i)

@@ -200,7 +200,7 @@ def tile_baller2vec_kernel(tc, x, pos, w_pos, b0, w1, b1, w2, b2, offs, out):
                             start=(m == 0),
                             stop=(m == MB - 1),
                         )
-                    if s < 2 or (s * DB + d) % 3 == 0:
+                    if s < 2 or (d % 2 == 0 if s >= OPEN else (s * DB + d) % 3 == 0):
                         nc.scalar.activation(
                             staged[:, k, :], acc_out[:, :width], IDENTITY, bias=b2_scaled[:, d : d + 1], scale=SCALE
                         )

import math

import concourse.mybir as mybir
from concourse.masks import make_identity

F32, BF16, U16 = mybir.dt.float32, mybir.dt.bfloat16, mybir.dt.uint16
ADD, SUB, MULT, MAX = mybir.AluOpType.add, mybir.AluOpType.subtract, mybir.AluOpType.mult, mybir.AluOpType.max
IDENTITY, RELU = mybir.ActivationFunctionType.Identity, mybir.ActivationFunctionType.Relu

P = 128
C, S, N, Q, M1, D = 256, 4096, 2048, 3, 256, 512
SCALE = math.sqrt(D)
CB, MB, DB = C // P, M1 // P, D // P
PIECE = 512
PIECES = N // PIECE
CHUNKS = N // P
PARTS = 3
ROWS = PARTS * PARTS * Q
POS_ROWS = 64
WIDTHS = (PIECE // 2, PIECE // 2, PIECE, PIECE, PIECE // 2, PIECE // 2)
STARTS = tuple(sum(WIDTHS[:s]) for s in range(len(WIDTHS)))
STEPS = len(WIDTHS)
PARTS_0 = (PIECE // 2, PIECE // 2, PIECE, PIECE, PIECE)
STARTS_0 = tuple(sum(PARTS_0[:i]) for i in range(len(PARTS_0)))
LAST_0 = len(PARTS_0) - 1
OPEN = 4
FLOPS = 2 * N * (C * Q + C * M1 + M1 * D)


def tile_baller2vec_kernel(tc, x, pos, w_pos, b0, w1, b1, w2, b2, offs, out):
    nc = tc.nc
    with (
        tc.tile_pool(name="held", bufs=1) as held,
        tc.tile_pool(name="work", bufs=6) as work,
        tc.tile_pool(name="ring", bufs=2) as ring,
        tc.tile_pool(name="ring_other", bufs=4) as ring_other,
        tc.tile_pool(name="stage", bufs=16) as stage,
        tc.psum_pool(name="psum", bufs=8) as psum,
    ):
        ident = held.tile([P, P], BF16, name="ident")
        make_identity(nc, ident[:])

        pos_parts = held.tile([P, CHUNKS, P], BF16, name="pos_parts")
        nc.vector.memset(pos_parts[:], 0.0)
        w_parts = held.tile([P, CB, P], BF16, name="w_parts")
        nc.gpsimd.memset(w_parts[:], 0.0)
        ident_f32 = held.tile([POS_ROWS, POS_ROWS], F32, name="ident_f32")
        nc.vector.tensor_copy(ident_f32[:], ident[:POS_ROWS, :POS_ROWS])

        x_blocks = x.rearrange("(p b) s -> b p s", b=CB)
        pos_sb = held.tile([POS_ROWS, P], F32, name="pos_sb")
        pos_rows = pos.rearrange("q (k t) -> (q k) t", t=P)
        nc.sync.dma_start(pos_sb[0:32, :], pos_rows[0:32, :])
        nc.sync.dma_start(pos_sb[32:48, :], pos_rows[32:48, :])
        nc.sync.dma_start(pos_sb[48:64, :], pos_rows[32:48, :])
        wpos_sb = held.tile([P, CB, Q], F32, name="wpos_sb")
        nc.sync.dma_start(wpos_sb[:], w_pos.rearrange("(p b) q -> p b q", b=CB))
        offsets = held.tile([P, N // 16], U16, name="offsets")
        nc.sync.dma_start(offsets[:], offs)
        b0_sb = held.tile([P, CB], F32, name="b0_sb")
        b1_sb = held.tile([P, MB], F32, name="b1_sb")
        b2_sb = held.tile([P, DB], F32, name="b2_sb")
        with nc.allow_non_contiguous_dma(reason="a bias: one element to a partition"):
            nc.sync.dma_start(b0_sb[:], b0.rearrange("(p b) o -> p (b o)", b=CB))
        x_sb = [held.tile([P, S], F32, name=f"x_sb{b}") for b in range(CB)]
        nc.sync.dma_start(x_sb[0][:], x_blocks[0, :, :])
        w1_sb = held.tile([P, CB, M1], BF16, name="w1_sb")
        nc.sync.dma_start(w1_sb[:], w1.rearrange("(p b) m -> p b m", b=CB))
        nc.sync.dma_start(x_sb[1][:], x_blocks[1, :, :])
        with nc.allow_non_contiguous_dma(reason="a bias: one element to a partition"):
            nc.sync.dma_start(b1_sb[:], b1.rearrange("(b p) o -> p (b o)", p=P))
            nc.sync.dma_start(b2_sb[:], b2.rearrange("(b p) o -> p (b o)", p=P))
        w2_sb = held.tile([P, MB, D], BF16, name="w2_sb")
        nc.sync.dma_start(w2_sb[:], w2.rearrange("(b p) d -> p b d", p=P))

        w_cols = w_parts[:, :, :ROWS].rearrange("p k (a b q) -> p k a b q", a=PARTS, b=PARTS)
        w_rest = held.tile([P, CB, Q], F32, name="w_rest")

        def to_all_a(ap):
            return ap.unsqueeze(2).to_broadcast([P, CB, PARTS, Q])

        nc.gpsimd.tensor_copy(w_cols[:, :, :, 0, :], to_all_a(wpos_sb[:]))
        nc.gpsimd.tensor_tensor(w_cols[:, :, :, 1, :], to_all_a(wpos_sb[:]), w_cols[:, :, :, 0, :], SUB)
        nc.gpsimd.tensor_tensor(w_rest[:], wpos_sb[:], w_cols[:, :, 0, 0, :], SUB)
        nc.gpsimd.tensor_tensor(w_cols[:, :, :, 2, :], to_all_a(w_rest[:]), w_cols[:, :, :, 1, :], SUB)

        flipped_pos = psum.tile([P, PIECE], F32, name="bank")
        nc.tensor.transpose(flipped_pos[:, :POS_ROWS], pos_sb[:], ident_f32[:])
        pos_tok = flipped_pos[:, : Q * CHUNKS].rearrange("p (q k) -> p k q", q=Q)
        p_cols = pos_parts[:, :, :ROWS].rearrange("p k (a b q) -> p k a b q", a=PARTS, b=PARTS)
        p_rest = held.tile([P, CHUNKS, Q], F32, name="p_rest")

        def split_pos(chunks):
            def to_all_b(ap):
                return ap.unsqueeze(2).to_broadcast([P, chunks.stop - chunks.start, PARTS, Q])

            tok, rest, cols = pos_tok[:, chunks, :], p_rest[:, chunks, :], p_cols[:, chunks, :, :, :]
            nc.vector.tensor_copy(cols[:, :, 0, :, :], to_all_b(tok))
            nc.vector.tensor_tensor(cols[:, :, 1, :, :], to_all_b(tok), cols[:, :, 0, :, :], SUB)
            nc.vector.tensor_tensor(rest, tok, cols[:, :, 0, 0, :], SUB)
            nc.vector.tensor_tensor(cols[:, :, 2, :, :], to_all_b(rest), cols[:, :, 1, :, :], SUB)

        w_rows = held.tile([P, C], BF16, name="w_rows")
        flipped_w = psum.tile([P, 2 * PIECE], BF16, name="bank")
        for b in range(CB):
            nc.tensor.transpose(flipped_w[:, b * P : (b + 1) * P], w_parts[:, b, :], ident[:])
        nc.scalar.copy(w_rows[:], flipped_w[:, :C])

        p_rows = held.tile([P, N], BF16, name="p_rows")
        first_piece = slice(0, PIECE // P)
        split_pos(first_piece)

        def flip_pos(p):
            flipped = psum.tile([P, 2 * PIECE], BF16, name="bank")
            for k in range(PIECE // P):
                nc.tensor.transpose(flipped[:, k * P : (k + 1) * P], pos_parts[:, p * (PIECE // P) + k, :], ident[:])
            if p == 0:
                nc.scalar.copy(p_rows[:, :PIECE], flipped[:, :PIECE])
            else:
                nc.vector.tensor_copy(p_rows[:, p * PIECE : (p + 1) * PIECE], flipped[:, :PIECE])

        flip_pos(0)
        split_pos(slice(PIECE // P, CHUNKS))
        for p in range(1, PIECES):
            flip_pos(p)

        b2_scaled = held.tile([P, DB], F32, name="b2_scaled")
        nc.gpsimd.tensor_scalar(b2_scaled[:], b2_sb[:], SCALE, None, MULT)

        other_sb = {}
        h0 = {}
        h1 = [held.tile([P, MB, WIDTHS[s]], BF16, name=f"h1_{s}") for s in range(STEPS)]

        def make_other(b, i):
            width = PARTS_0[i]
            cols = slice(STARTS_0[i], STARTS_0[i] + width)
            acc_other = psum.tile([P, PIECE], F32, name="bank")
            nc.tensor.matmul(acc_other[:, :width], w_rows[:, b * P : (b + 1) * P], p_rows[:, cols], start=True, stop=True)
            other_sb[b, i] = (work if b == 0 else ring_other).tile([P, PIECE], F32, name=f"other{b}")
            nc.scalar.activation(other_sb[b, i][:, :width], acc_other[:, :width], IDENTITY, bias=b0_sb[:, b : b + 1])

        summed = {}

        def look_up(b, s):
            width = PARTS_0[s] if b == 0 else WIDTHS[s]
            start = STARTS_0[s] if b == 0 else STARTS[s]
            step_offsets = offsets[:, start // 16 : (start + width) // 16]
            i = min(s, LAST_0)
            within = slice(start - STARTS_0[i], start - STARTS_0[i] + width)
            if b == 0:
                summed[b, s] = work.tile([P, PIECE], F32, name="summed0")
            elif WIDTHS[s] < PIECE:
                summed[b, s] = held.tile([P, PIECE], F32, name=f"summed1_{s}")
            else:
                summed[b, s] = held.tile([P, PIECE], F32, name="summed1_full")
            nc.vector.tensor_tensor(summed[b, s][:, :width], x_sb[b][:].indirect(step_offsets), other_sb[b, i][:, within], ADD)

        def relu_h0(b, s):
            h0[b, s] = (work if b == 0 else ring).tile([P, PIECE], BF16, name=f"h0_{b}")
            width = PARTS_0[s] if b == 0 else WIDTHS[s]
            if (s < OPEN) if b == 0 else (WIDTHS[s] < PIECE):
                nc.scalar.activation(h0[b, s][:, :width], summed[b, s][:, :width], RELU)
            else:
                nc.vector.tensor_scalar(h0[b, s][:, :width], summed[b, s][:, :width], 0.0, None, MAX)

        acc_h1 = {}

        def layer1_block0(s):
            acc_h1[s] = [psum.tile([P, PIECE], F32, name="bank") for m in range(MB)]
            i = min(s, LAST_0)
            within = slice(STARTS[s] - STARTS_0[i], STARTS[s] - STARTS_0[i] + WIDTHS[s])
            for m in range(MB):
                nc.tensor.matmul(
                    acc_h1[s][m][:, : WIDTHS[s]], w1_sb[:, 0, m * P : (m + 1) * P], h0[0, i][:, within], start=True, stop=False
                )

        def layer1_block1(s):
            if s >= OPEN:
                layer1_block0(s)
            for m in range(MB):
                nc.tensor.matmul(
                    acc_h1[s][m][:, : WIDTHS[s]], w1_sb[:, 1, m * P : (m + 1) * P], h0[1, s][:, : WIDTHS[s]], start=False, stop=True
                )
                nc.scalar.activation(h1[s][:, m, :], acc_h1[s][m][:, : WIDTHS[s]], RELU, bias=b1_sb[:, m : m + 1])

        def layer2(s):
            width = WIDTHS[s]
            cols = slice(STARTS[s], STARTS[s] + width)
            together = 2 if s >= OPEN else 1
            for first in range(0, DB, together):
                staged = stage.tile([P, together, width], F32, name=f"staged{together}")
                for k in range(together):
                    d = first + k
                    acc_out = psum.tile([P, PIECE], F32, name="bank")
                    for m in range(MB):
                        nc.tensor.matmul(
                            acc_out[:, :width],
                            w2_sb[:, m, d * P : (d + 1) * P],
                            h1[s][:, m, :],
                            start=(m == 0),
                            stop=(m == MB - 1),
                        )
                    if s < 2 or (d % 2 == 0 if s >= OPEN else (s * DB + d) % 3 == 0):
                        nc.scalar.activation(
                            staged[:, k, :], acc_out[:, :width], IDENTITY, bias=b2_scaled[:, d : d + 1], scale=SCALE
                        )
                    else:
                        nc.vector.tensor_scalar(
                            staged[:, k, :], acc_out[:, :width], SCALE, b2_scaled[:, d : d + 1], MULT, ADD
                        )
                rows = out[first * P : (first + together) * P, cols]
                nc.sync.dma_start(rows.rearrange("(k p) n -> p k n", p=P), staged[:])

        for i in range(LAST_0 + 1):
            make_other(0, i)
        for s in range(LAST_0 + 1):
            look_up(0, s)
            if s < OPEN:
                relu_h0(0, s)
                make_other(1, s)
        for s in range(OPEN):
            layer1_block0(s)
        for t in range(STEPS + 2):
            if t < STEPS:
                look_up(1, t)
                relu_h0(1, t)
            if 1 <= t <= STEPS:
                layer1_block1(t - 1)
            if t == 2:
                for i in range(OPEN, LAST_0 + 1):
                    make_other(1, i)
                    relu_h0(0, i)
            if t >= 2:
                layer2(t - 2)
